import numpy as np
import ml_dtypes


def mxq(x, axis, fmt="e4m3"):
    dtype, down = {"e4m3": (ml_dtypes.float8_e4m3fn, 7), "e5m2": (ml_dtypes.float8_e5m2, 14)}[fmt]
    v = np.moveaxis(np.asarray(x, np.float32).astype(ml_dtypes.bfloat16).astype(np.float64), axis, -1)
    blocks = v.reshape(v.shape[:-1] + (-1, 32))
    amax = np.abs(blocks).max(-1, keepdims=True)
    byte = np.maximum(np.where(amax > 0, np.frexp(amax)[1] - 1 + 127, 0) - down, 1)
    scale = np.exp2(byte - 127.0)
    codes = (blocks / scale).astype(np.float32).astype(dtype).astype(np.float64)
    return np.moveaxis((codes * scale).reshape(v.shape), -1, axis)


WIDE = False


def mx_kscale(k):
    if not WIDE:
        return np.ones(k)
    levels = np.array([10, -10, 5, -5, 0])
    a = np.random.permutation(np.resize(levels, k // 512 * 4)).reshape(k // 512, 4)
    idx = np.arange(k)
    return np.exp2(a[idx // 512, idx % 128 // 32])


BF16 = ml_dtypes.bfloat16


def bf(x):
    return np.asarray(x, np.float32).astype(BF16)


def f64(x):
    return np.asarray(x).astype(np.float64)


N, NB, D = 4096, 1024, 1024

INV_SQRT_2PI = 1.0 / np.sqrt(2.0 * np.pi)


def phi(t):
    return INV_SQRT_2PI * np.exp(-0.5 * t * t)


def setup_inputs():
    a = np.log2(mx_kscale(NB))
    u = np.exp2(np.round(1.2 * (a - a.min())))
    g = np.where(u > 1.0, np.where(u == u.max(), 0.25, 0.1), 1.0)
    q_mu = 0.5 + 0.2 * np.random.standard_normal(N)
    q_sigma_sq = 0.01 + 0.1 * np.random.random(N)
    theta = np.stack([q_mu / q_sigma_sq, -0.5 / q_sigma_sq], axis=1)
    basis_mu = np.linspace(0.0, 1.0, NB) + 0.01 * np.random.standard_normal(NB)
    basis_sigma = 0.05 * (1.0 + 0.1 * np.random.standard_normal(NB)) * u
    Bv = np.random.standard_normal((NB, D)) * 0.64 / np.sqrt(NB) * (u * g)[:, None]
    return {"theta": bf(theta), "basis_mu": bf(basis_mu), "basis_sigma": bf(basis_sigma), "Bv": bf(Bv)}


def reference(theta, basis_mu, basis_sigma, Bv):
    theta, basis_mu, basis_sigma, Bv = f64(theta), f64(basis_mu), f64(basis_sigma), f64(Bv)
    sigma_sq = -0.5 / theta[:, 1]
    mu = theta[:, 0] * sigma_sq
    s = np.sqrt(basis_sigma[None, :] ** 2 + sigma_sq[:, None])
    r = phi((mu[:, None] - basis_mu[None, :]) / s) / s
    context = mxq(r, 1, "e4m3") @ mxq(Bv, 0, "e4m3")
    return context

@@ -1,0 +1,292 @@
+import math
+from contextlib import ExitStack
+
+import concourse.mybir as mybir
+from concourse.masks import make_identity
+
+F32 = mybir.dt.float32
+BF16 = mybir.dt.bfloat16
+U32 = mybir.dt.uint32
+U8 = mybir.dt.uint8
+FP8X4 = mybir.dt.float8_e4m3fn_x4
+AF = mybir.ActivationFunctionType
+ALU = mybir.AluOpType
+
+P = 128
+ROWS, NB, D = 4096, 1024, 1024
+PACK = 4
+PASSES = NB // (P * PACK)
+TILES = ROWS // P
+CHUNK_TILES = 4
+CHUNK = CHUNK_TILES * P
+CHUNKS = TILES // CHUNK_TILES
+UNITS = CHUNKS * PASSES
+BANK = 512
+
+FLOPS = 2 * ROWS * NB * D
+
+GROUPS = ((0, 4), (4, 8), (8, 12), (12, 16))
+Z_ON_POOL = True
+EV_PER_UNIT = 4
+ACT_EV = ()
+LL_BUFS = 9
+WW_BUFS = 6
+
+
+def plan():
+    steps = []
+    pending = []
+    taken = [0]
+    done = {}
+    issued = {}
+
+    def drain(k, act_slots):
+        for s in range(min(k, len(pending) - taken[0])):
+            h, a, dh = pending[taken[0]]
+            taken[0] += 1
+            steps.append(("EV", h, a, dh, "act" if s in act_slots else "dve"))
+            done[(h, a // 2)] = done.get((h, a // 2), 0) + 1
+            if done[(h, a // 2)] == 4:
+                steps.append(("ST", h, a // 2))
+
+    def bcast(kind, h):
+        if h < CHUNKS and (kind, h) not in issued:
+            issued[(kind, h)] = 1
+            steps.append((kind, h))
+
+    def logs(lo, hi):
+        for u in range(lo, hi):
+            bcast("BR", u // 2)
+            steps.append(("LN", u))
+            if u % 2 == 1:
+                bcast("BR", u // 2 + 1)
+
+    def finish(u):
+        steps.append(("F", u))
+
+    def quant(u):
+        steps.append(("Q", u))
+        if u % 2 == 1:
+            for a in range(CHUNK_TILES):
+                steps.append(("MX", u // 2, a))
+                pending.append((u // 2, a, 0))
+                pending.append((u // 2, a, 1))
+
+    logs(GROUPS[0][0], GROUPS[0][1])
+    for gi in range(len(GROUPS)):
+        lo, hi = GROUPS[gi]
+        prev = list(range(GROUPS[gi - 1][0], GROUPS[gi - 1][1])) if gi > 0 else []
+        for idx in range(hi - lo):
+            u = lo + idx
+            bcast("BM", u // 2)
+            steps.append(("W", u))
+            if idx < len(prev):
+                finish(prev[idx])
+            steps.append(("A1", u))
+            steps.append(("B2", u))
+            if idx < len(prev):
+                quant(prev[idx])
+            steps.append(("Z", u))
+            if u % 2 == 1:
+                bcast("BM", u // 2 + 1)
+            drain(EV_PER_UNIT, ACT_EV)
+            if gi == 0 and idx < 2:
+                steps.append(("BVG", idx))
+            if gi == 0 and 1 <= idx < 3:
+                steps.append(("BVQ", idx - 1))
+        if gi + 1 < len(GROUPS):
+            logs(GROUPS[gi + 1][0], GROUPS[gi + 1][1])
+    for u in range(GROUPS[-1][0], GROUPS[-1][1]):
+        finish(u)
+        drain(2, (0,))
+        quant(u)
+    while taken[0] < len(pending):
+        drain(2, (1,))
+    return steps
+
+
+def tile_longtermattention_kernel(tc, theta, basis_mu, basis_sigma, Bv, out):
+    nc = tc.nc
+    out_v = out.rearrange("(p i) d -> p i d", i=TILES)
+    kappa = math.sqrt(2.0 * math.pi)
+    with ExitStack() as ctx:
+        ctx.enter_context(tc.manual_schedule())
+        const = ctx.enter_context(tc.tile_pool(name="const", bufs=1))
+        llp = ctx.enter_context(tc.tile_pool(name="llp", bufs=LL_BUFS))
+        wwp = ctx.enter_context(tc.tile_pool(name="wwp", bufs=WW_BUFS))
+        rbp = ctx.enter_context(tc.tile_pool(name="rbp", bufs=3))
+        qp = ctx.enter_context(tc.tile_pool(name="qp", bufs=6))
+        op = ctx.enter_context(tc.tile_pool(name="op", bufs=4))
+        bps = ctx.enter_context(tc.psum_pool(name="bps", bufs=2))
+        aps = ctx.enter_context(tc.psum_pool(name="aps", bufs=4))
+
+        th = const.tile([P, TILES, 2], BF16)
+        nc.sync.dma_start(out=th[:], in_=theta.rearrange("(p i) two -> p i two", i=TILES))
+        bs = const.tile([P, PASSES, PACK], BF16)
+        nc.sync.dma_start(out=bs[:], in_=basis_sigma.rearrange("(c p t) -> p c t", p=P, t=PACK))
+        bm = const.tile([P, PASSES, PACK], BF16)
+        nc.sync.dma_start(out=bm[:], in_=basis_mu.rearrange("(c p t) -> p c t", p=P, t=PACK))
+        raws = []
+        for c in range(PASSES):
+            raw = llp.tile([P, PACK, D], BF16, tag="ll", align_bytes=64)
+            nc.sync.dma_start(
+                out=raw[:],
+                in_=Bv[c * P * PACK : (c + 1) * P * PACK, :].rearrange("(p t) w -> p t w", t=PACK),
+            )
+            raws.append(raw)
+
+        ident = const.tile([P, P], F32)
+        make_identity(nc, ident[:])
+
+        warm = const.tile([P, 1], F32)
+        nc.vector.memset(warm[:], 1.0)
+        warm2 = const.tile([P, 1], F32)
+        nc.scalar.activation(out=warm2[:], in_=warm[:], func=AF.Ln)
+
+        rec = const.tile([P, TILES], F32)
+        nc.vector.reciprocal(out=rec[:], in_=th[:, :, 1])
+        mu = const.tile([P, TILES], F32)
+        nc.vector.scalar_tensor_tensor(
+            out=mu[:], in0=rec[:], scalar=-0.5 * kappa, in1=th[:, :, 0], op0=ALU.mult, op1=ALU.mult
+        )
+        bsf = bs[:].rearrange("p c t -> p (c t)")
+        b2 = const.tile([P, PASSES * PACK], F32)
+        nc.vector.scalar_tensor_tensor(
+            out=b2[:], in0=bsf, scalar=2.0 * math.pi, in1=bsf, op0=ALU.mult, op1=ALU.mult
+        )
+        bmf = const.tile([P, PASSES * PACK], F32)
+        nc.vector.tensor_scalar_mul(out=bmf[:], in0=bm[:].rearrange("p c t -> p (c t)"), scalar1=kappa)
+
+        bvc = const.tile([P, PASSES, D], U32, align_bytes=64)
+        bvs = const.tile([P, PASSES, D], U8, align_bytes=64)
+
+        recb, mub, ll, ww, rb, cod, scl, acc, ost, grp = {}, {}, {}, {}, {}, {}, {}, {}, {}, {}
+
+        for st in plan():
+            kind = st[0]
+            if kind == "BR" or kind == "BM":
+                h = st[1]
+                src = rec if kind == "BR" else mu
+                bk = bps.tile([P, BANK], F32, tag=kind)
+                for a in range(CHUNK_TILES):
+                    i = h * CHUNK_TILES + a
+                    nc.tensor.matmul(
+                        out=bk[:, a * P : (a + 1) * P],
+                        lhsT=src[:, i : i + 1].to_broadcast([P, P]),
+                        rhs=ident[:],
+                        start=True,
+                        stop=True,
+                    )
+                if kind == "BR":
+                    recb[h] = bk
+                else:
+                    mub[h] = bk
+            elif kind == "LN":
+                u = st[1]
+                lt = llp.tile([P, PACK, CHUNK], F32, tag="ll", align_bytes=64)
+                for t in range(PACK):
+                    k = (u % 2) * PACK + t
+                    nc.scalar.activation(
+                        out=lt[:, t, :],
+                        in_=recb[u // 2][:],
+                        func=AF.Ln,
+                        bias=b2[:, k : k + 1],
+                        scale=-math.pi,
+                    )
+                ll[u] = lt
+            elif kind == "W":
+                u = st[1]
+                wt = wwp.tile([P, PACK, CHUNK], F32, tag="ww", align_bytes=64)
+                nc.scalar.activation(
+                    out=wt[:].rearrange("p t n -> p (t n)"),
+                    in_=ll[u][:].rearrange("p t n -> p (t n)"),
+                    func=AF.Exp,
+                    scale=-1.0,
+                )
+                ww[u] = wt
+            elif kind == "A1" or kind == "B2":
+                u = st[1]
+                for t in range(PACK):
+                    k = (u % 2) * PACK + t
+                    nc.vector.scalar_tensor_tensor(
+                        out=ww[u][:, t, :],
+                        in0=mub[u // 2][:],
+                        scalar=bmf[:, k : k + 1],
+                        in1=ww[u][:, t, :],
+                        op0=ALU.subtract,
+                        op1=ALU.mult,
+                    )
+            elif kind == "Z":
+                u = st[1]
+                wf = ww[u][:].rearrange("p t n -> p (t n)")
+                lf = ll[u][:].rearrange("p t n -> p (t n)")
+                if Z_ON_POOL:
+                    nc.gpsimd.tensor_tensor(out=wf, in0=wf, in1=lf, op=ALU.add)
+                else:
+                    nc.vector.tensor_tensor(out=wf, in0=wf, in1=lf, op=ALU.add)
+            elif kind == "F":
+                u = st[1]
+                rbt = rbp.tile([P, CHUNK, PACK], BF16, align_bytes=64)
+                nc.scalar.activation(
+                    out=rbt[:].rearrange("p (m i) t -> p m t i", i=4),
+                    in_=ww[u][:].rearrange("p t (m i) -> p m t i", i=4),
+                    func=AF.Exp,
+                    scale=-0.5,
+                )
+                rb[u] = rbt
+            elif kind == "Q":
+                u = st[1]
+                cdt = qp.tile([P, CHUNK], U32, align_bytes=64)
+                sct = qp.tile([P, CHUNK], U8, align_bytes=64)
+                nc.vector.quantize_mx(
+                    out=cdt[:].bitcast(FP8X4),
+                    scales=sct[:],
+                    in_=rb[u][:].rearrange("p n t -> p (n t)"),
+                )
+                cod[u], scl[u] = cdt, sct
+            elif kind == "BVG":
+                c = st[1]
+                gt = wwp.tile([P, D, PACK], BF16, tag="ww", align_bytes=64)
+                nc.vector.tensor_copy(
+                    out=gt[:].rearrange("p (m i) t -> p m t i", i=4),
+                    in_=raws[c][:].rearrange("p t (m i) -> p m t i", i=4),
+                )
+                grp[c] = gt
+            elif kind == "BVQ":
+                c = st[1]
+                nc.vector.quantize_mx(
+                    out=bvc[:, c, :].bitcast(FP8X4),
+                    scales=bvs[:, c, :],
+                    in_=grp[c][:].rearrange("p w t -> p (w t)"),
+                )
+            elif kind == "MX":
+                h, a = st[1], st[2]
+                cols = slice(a * P, (a + 1) * P)
+                for dh in range(D // BANK):
+                    at = aps.tile([P, BANK], F32, tag="acc")
+                    dcols = slice(dh * BANK, (dh + 1) * BANK)
+                    for c in range(PASSES):
+                        nc.tensor.matmul_mx(
+                            out=at[:],
+                            lhsT=cod[2 * h + c][:, cols].bitcast(FP8X4),
+                            lhsT_scale=scl[2 * h + c][:, cols],
+                            rhs=bvc[:, c, dcols].bitcast(FP8X4),
+                            rhs_scale=bvs[:, c, dcols],
+                            start=(c == 0),
+                            stop=(c == PASSES - 1),
+                        )
+                    acc[(h, a, dh)] = at
+            elif kind == "EV":
+                h, a, dh, eng = st[1], st[2], st[3], st[4]
+                if (h, a // 2) not in ost:
+                    ot = op.tile([P, 2, D], F32)
+                    ost[(h, a // 2)] = ot
+                dst = ost[(h, a // 2)][:, a % 2, dh * BANK : (dh + 1) * BANK]
+                if eng == "act":
+                    nc.scalar.copy(out=dst, in_=acc[(h, a, dh)][:])
+                else:
+                    nc.vector.tensor_copy(out=dst, in_=acc[(h, a, dh)][:])
+            elif kind == "ST":
+                h, half = st[1], st[2]
+                i0 = h * CHUNK_TILES + 2 * half
+                nc.sync.dma_start(out=out_v[:, i0 : i0 + 2, :], in_=ost[(h, half)][:])

@@ -26,11 +26,15 @@ BANK = 512
 FLOPS = 2 * ROWS * NB * D
 
 GROUPS = ((0, 4), (4, 8), (8, 12), (12, 16))
-Z_ON_POOL = True
-EV_PER_UNIT = 4
-ACT_EV = ()
-LL_BUFS = 9
+Z_ON_DVE = (15,)
+SPLIT_UNITS = (15,)
+LL_BUFS = 8
 WW_BUFS = 6
+EV_DVE = (4, 4, 4, 0)
+EV_ACT = (0, 0, 0, 2)
+TAIL_ACT0 = 6
+TAIL_ACT = 0
+TAIL_DVE = 1
 
 
 def plan():
@@ -40,11 +44,14 @@ def plan():
     done = {}
     issued = {}
 
-    def drain(k, act_slots):
-        for s in range(min(k, len(pending) - taken[0])):
+    def drain(n_dve, n_act):
+        order = ["act"] * n_act + ["dve"] * n_dve
+        for eng in order:
+            if taken[0] >= len(pending):
+                return
             h, a, dh = pending[taken[0]]
             taken[0] += 1
-            steps.append(("EV", h, a, dh, "act" if s in act_slots else "dve"))
+            steps.append(("EV", h, a, dh, eng))
             done[(h, a // 2)] = done.get((h, a // 2), 0) + 1
             if done[(h, a // 2)] == 4:
                 steps.append(("ST", h, a // 2))
@@ -54,54 +61,67 @@ def plan():
             issued[(kind, h)] = 1
             steps.append((kind, h))
 
+    def mx(h, a):
+        steps.append(("MX", h, a))
+        pending.append((h, a, 0))
+        pending.append((h, a, 1))
+
     def logs(lo, hi):
         for u in range(lo, hi):
             bcast("BR", u // 2)
             steps.append(("LN", u))
             if u % 2 == 1:
-                bcast("BR", u // 2 + 1)
+                bcast("BR", u // 2 + 2)
 
-    def finish(u):
-        steps.append(("F", u))
-
-    def quant(u):
-        steps.append(("Q", u))
-        if u % 2 == 1:
-            for a in range(CHUNK_TILES):
-                steps.append(("MX", u // 2, a))
-                pending.append((u // 2, a, 0))
-                pending.append((u // 2, a, 1))
-
+    bcast("BR", 0)
+    bcast("BR", 1)
+    bcast("BM", 0)
+    bcast("BM", 1)
+    steps.append(("BVG", 0))
+    steps.append(("BVG", 1))
+    steps.append(("BVQ", 0))
+    steps.append(("BVQ", 1))
     logs(GROUPS[0][0], GROUPS[0][1])
     for gi in range(len(GROUPS)):
         lo, hi = GROUPS[gi]
         prev = list(range(GROUPS[gi - 1][0], GROUPS[gi - 1][1])) if gi > 0 else []
-        for idx in range(hi - lo):
-            u = lo + idx
-            bcast("BM", u // 2)
-            steps.append(("W", u))
-            if idx < len(prev):
-                finish(prev[idx])
-            steps.append(("A1", u))
-            steps.append(("B2", u))
-            if idx < len(prev):
-                quant(prev[idx])
-            steps.append(("Z", u))
-            if u % 2 == 1:
-                bcast("BM", u // 2 + 1)
-            drain(EV_PER_UNIT, ACT_EV)
-            if gi == 0 and idx < 2:
-                steps.append(("BVG", idx))
-            if gi == 0 and 1 <= idx < 3:
-                steps.append(("BVQ", idx - 1))
-        if gi + 1 < len(GROUPS):
+        last = gi + 1 == len(GROUPS)
+        for idx in range(max(hi - lo, len(prev))):
+            u = lo + idx if idx < hi - lo else None
+            p = prev[idx] if idx < len(prev) else None
+            if u is not None:
+                steps.append(("W", u))
+            if p is not None:
+                steps.append(("F", p, 0, CHUNK_TILES))
+            if u is not None:
+                steps.append(("A1", u))
+                steps.append(("B2", u))
+                if u % 2 == 1:
+                    bcast("BM", u // 2 + 2)
+            drain(0, EV_ACT[gi])
+            if p is not None:
+                steps.append(("Q", p, 0, CHUNK_TILES))
+            if u is not None:
+                steps.append(("Z", u, "dve" if u in Z_ON_DVE else "pool"))
+            drain(EV_DVE[gi], 0)
+            if p is not None and p % 2 == 1:
+                for a in range(CHUNK_TILES):
+                    mx(p // 2, a)
+        if not last:
             logs(GROUPS[gi + 1][0], GROUPS[gi + 1][1])
+    drain(0, TAIL_ACT0)
     for u in range(GROUPS[-1][0], GROUPS[-1][1]):
-        finish(u)
-        drain(2, (0,))
-        quant(u)
+        parts = CHUNK_TILES if u in SPLIT_UNITS else 1
+        width = CHUNK_TILES // parts
+        for k in range(parts):
+            steps.append(("F", u, k * width, (k + 1) * width))
+            drain(TAIL_DVE * width, TAIL_ACT * width)
+            steps.append(("Q", u, k * width, (k + 1) * width))
+            if u % 2 == 1:
+                for a in range(k * width, (k + 1) * width):
+                    mx(u // 2, a)
     while taken[0] < len(pending):
-        drain(2, (1,))
+        drain(1, 1)
     return steps
 
 
@@ -220,30 +240,34 @@ def tile_longtermattention_kernel(tc, theta, basis_mu, basis_sigma, Bv, out):
                 u = st[1]
                 wf = ww[u][:].rearrange("p t n -> p (t n)")
                 lf = ll[u][:].rearrange("p t n -> p (t n)")
-                if Z_ON_POOL:
+                if st[2] == "pool":
                     nc.gpsimd.tensor_tensor(out=wf, in0=wf, in1=lf, op=ALU.add)
                 else:
                     nc.vector.tensor_tensor(out=wf, in0=wf, in1=lf, op=ALU.add)
             elif kind == "F":
                 u = st[1]
-                rbt = rbp.tile([P, CHUNK, PACK], BF16, align_bytes=64)
+                cols = slice(st[2] * P, st[3] * P)
+                if u not in rb:
+                    rbt = rbp.tile([P, CHUNK, PACK], BF16, align_bytes=64)
+                    rb[u] = rbt
                 nc.scalar.activation(
-                    out=rbt[:].rearrange("p (m i) t -> p m t i", i=4),
-                    in_=ww[u][:].rearrange("p t (m i) -> p m t i", i=4),
+                    out=rb[u][:, cols, :].rearrange("p (m i) t -> p m t i", i=4),
+                    in_=ww[u][:, :, cols].rearrange("p t (m i) -> p m t i", i=4),
                     func=AF.Exp,
                     scale=-0.5,
                 )
-                rb[u] = rbt
             elif kind == "Q":
                 u = st[1]
-                cdt = qp.tile([P, CHUNK], U32, align_bytes=64)
-                sct = qp.tile([P, CHUNK], U8, align_bytes=64)
+                cols = slice(st[2] * P, st[3] * P)
+                if u not in cod:
+                    cdt = qp.tile([P, CHUNK], U32, align_bytes=64)
+                    sct = qp.tile([P, CHUNK], U8, align_bytes=64)
+                    cod[u], scl[u] = cdt, sct
                 nc.vector.quantize_mx(
-                    out=cdt[:].bitcast(FP8X4),
-                    scales=sct[:],
-                    in_=rb[u][:].rearrange("p n t -> p (n t)"),
+                    out=cod[u][:, cols].bitcast(FP8X4),
+                    scales=scl[u][:, cols],
+                    in_=rb[u][:, cols, :].rearrange("p n t -> p (n t)"),
                 )
-                cod[u], scl[u] = cdt, sct
             elif kind == "BVG":
                 c = st[1]
                 gt = wwp.tile([P, D, PACK], BF16, tag="ww", align_bytes=64)

@@ -22,106 +22,89 @@ CHUNK = CHUNK_TILES * P
 CHUNKS = TILES // CHUNK_TILES
 UNITS = CHUNKS * PASSES
 BANK = 512
+GROUP = 4
+GROUPS = UNITS // GROUP
 
 FLOPS = 2 * ROWS * NB * D
 
-GROUPS = ((0, 4), (4, 8), (8, 12), (12, 16))
-Z_ON_DVE = (15,)
-SPLIT_UNITS = (15,)
-LL_BUFS = 8
-WW_BUFS = 6
-EV_DVE = (4, 4, 4, 0)
-EV_ACT = (0, 0, 0, 2)
-TAIL_ACT0 = 6
-TAIL_ACT = 0
-TAIL_DVE = 1
+VECTOR_BANKS_A_UNIT = 4
+SCALAR_BANKS_A_UNIT = 2
+SCALAR_BANKS_BEFORE_THE_END = 6
+LAST_UNIT = UNITS - 1
 
 
 def plan():
     steps = []
-    pending = []
-    taken = [0]
-    done = {}
-    issued = {}
+    banks = []
+    emptied = [0]
+    copied = {}
 
-    def drain(n_dve, n_act):
-        order = ["act"] * n_act + ["dve"] * n_dve
-        for eng in order:
-            if taken[0] >= len(pending):
-                return
-            h, a, dh = pending[taken[0]]
-            taken[0] += 1
-            steps.append(("EV", h, a, dh, eng))
-            done[(h, a // 2)] = done.get((h, a // 2), 0) + 1
-            if done[(h, a // 2)] == 4:
-                steps.append(("ST", h, a // 2))
+    def empty(count, engine):
+        for s in range(min(count, len(banks) - emptied[0])):
+            h, a, half = banks[emptied[0]]
+            emptied[0] += 1
+            steps.append(("EV", h, a, half, engine))
+            tiles = 1 if h == CHUNKS - 1 else 2
+            first = a - a % tiles
+            copied[(h, first)] = copied.get((h, first), 0) + 1
+            if copied[(h, first)] == 2 * tiles:
+                steps.append(("ST", h, first, first + tiles))
 
-    def bcast(kind, h):
-        if h < CHUNKS and (kind, h) not in issued:
-            issued[(kind, h)] = 1
-            steps.append((kind, h))
-
-    def mx(h, a):
+    def passes(h, a):
         steps.append(("MX", h, a))
-        pending.append((h, a, 0))
-        pending.append((h, a, 1))
+        banks.append((h, a, 0))
+        banks.append((h, a, 1))
 
-    def logs(lo, hi):
-        for u in range(lo, hi):
-            bcast("BR", u // 2)
+    def logarithms(group):
+        for u in range(group * GROUP, (group + 1) * GROUP):
             steps.append(("LN", u))
-            if u % 2 == 1:
-                bcast("BR", u // 2 + 2)
+            if u % 2 == 1 and u // 2 + 2 < CHUNKS:
+                steps.append(("BR", u // 2 + 2))
 
-    bcast("BR", 0)
-    bcast("BR", 1)
-    bcast("BM", 0)
-    bcast("BM", 1)
-    steps.append(("BVG", 0))
-    steps.append(("BVG", 1))
-    steps.append(("BVQ", 0))
-    steps.append(("BVQ", 1))
-    logs(GROUPS[0][0], GROUPS[0][1])
-    for gi in range(len(GROUPS)):
-        lo, hi = GROUPS[gi]
-        prev = list(range(GROUPS[gi - 1][0], GROUPS[gi - 1][1])) if gi > 0 else []
-        last = gi + 1 == len(GROUPS)
-        for idx in range(max(hi - lo, len(prev))):
-            u = lo + idx if idx < hi - lo else None
-            p = prev[idx] if idx < len(prev) else None
-            if u is not None:
-                steps.append(("W", u))
-            if p is not None:
-                steps.append(("F", p, 0, CHUNK_TILES))
-            if u is not None:
-                steps.append(("A1", u))
-                steps.append(("B2", u))
-                if u % 2 == 1:
-                    bcast("BM", u // 2 + 2)
-            drain(0, EV_ACT[gi])
-            if p is not None:
-                steps.append(("Q", p, 0, CHUNK_TILES))
-            if u is not None:
-                steps.append(("Z", u, "dve" if u in Z_ON_DVE else "pool"))
-            drain(EV_DVE[gi], 0)
-            if p is not None and p % 2 == 1:
+    for h in range(2):
+        steps.append(("BR", h))
+    for h in range(2):
+        steps.append(("BM", h))
+    for c in range(PASSES):
+        steps.append(("BVG", c))
+    for c in range(PASSES):
+        steps.append(("BVQ", c))
+    logarithms(0)
+    for group in range(GROUPS):
+        for u in range(group * GROUP, (group + 1) * GROUP):
+            before = u - GROUP
+            steps.append(("W", u))
+            if group > 0:
+                steps.append(("F", before, 0, CHUNK_TILES))
+            steps.append(("A1", u))
+            steps.append(("B2", u))
+            if u % 2 == 1 and u // 2 + 2 < CHUNKS:
+                steps.append(("BM", u // 2 + 2))
+            if group == GROUPS - 1:
+                empty(SCALAR_BANKS_A_UNIT, "act")
+            if group > 0:
+                steps.append(("Q", before, 0, CHUNK_TILES))
+            steps.append(("Z", u, "dve" if u == LAST_UNIT else "pool"))
+            if group < GROUPS - 1:
+                empty(VECTOR_BANKS_A_UNIT, "dve")
+            if group > 0 and before % 2 == 1:
                 for a in range(CHUNK_TILES):
-                    mx(p // 2, a)
-        if not last:
-            logs(GROUPS[gi + 1][0], GROUPS[gi + 1][1])
-    drain(0, TAIL_ACT0)
-    for u in range(GROUPS[-1][0], GROUPS[-1][1]):
-        parts = CHUNK_TILES if u in SPLIT_UNITS else 1
-        width = CHUNK_TILES // parts
-        for k in range(parts):
-            steps.append(("F", u, k * width, (k + 1) * width))
-            drain(TAIL_DVE * width, TAIL_ACT * width)
-            steps.append(("Q", u, k * width, (k + 1) * width))
+                    passes(before // 2, a)
+        if group < GROUPS - 1:
+            logarithms(group + 1)
+    empty(SCALAR_BANKS_BEFORE_THE_END, "act")
+    for u in range(UNITS - GROUP, UNITS):
+        width = 1 if u == LAST_UNIT else CHUNK_TILES
+        for a0 in range(0, CHUNK_TILES, width):
+            steps.append(("F", u, a0, a0 + width))
+            empty(width, "dve")
+            steps.append(("Q", u, a0, a0 + width))
             if u % 2 == 1:
-                for a in range(k * width, (k + 1) * width):
-                    mx(u // 2, a)
-    while taken[0] < len(pending):
-        drain(1, 1)
+                for a in range(a0, a0 + width):
+                    passes(u // 2, a)
+    while emptied[0] < len(banks):
+        empty(1, "act")
+        empty(1, "dve")
     return steps
 
 
@@ -132,13 +115,13 @@ def tile_longtermattention_kernel(tc, theta, basis_mu, basis_sigma, Bv, out):
     with ExitStack() as ctx:
         ctx.enter_context(tc.manual_schedule())
         const = ctx.enter_context(tc.tile_pool(name="const", bufs=1))
-        llp = ctx.enter_context(tc.tile_pool(name="llp", bufs=LL_BUFS))
-        wwp = ctx.enter_context(tc.tile_pool(name="wwp", bufs=WW_BUFS))
-        rbp = ctx.enter_context(tc.tile_pool(name="rbp", bufs=3))
-        qp = ctx.enter_context(tc.tile_pool(name="qp", bufs=6))
-        op = ctx.enter_context(tc.tile_pool(name="op", bufs=4))
-        bps = ctx.enter_context(tc.psum_pool(name="bps", bufs=2))
-        aps = ctx.enter_context(tc.psum_pool(name="aps", bufs=4))
+        logs = ctx.enter_context(tc.tile_pool(name="logs", bufs=8))
+        work = ctx.enter_context(tc.tile_pool(name="work", bufs=6))
+        rows = ctx.enter_context(tc.tile_pool(name="rows", bufs=3))
+        packed = ctx.enter_context(tc.tile_pool(name="packed", bufs=6))
+        results = ctx.enter_context(tc.tile_pool(name="results", bufs=4))
+        spread = ctx.enter_context(tc.psum_pool(name="spread", bufs=2))
+        sums = ctx.enter_context(tc.psum_pool(name="sums", bufs=4))
 
         th = const.tile([P, TILES, 2], BF16)
         nc.sync.dma_start(out=th[:], in_=theta.rearrange("(p i) two -> p i two", i=TILES))
@@ -148,7 +131,7 @@ def tile_longtermattention_kernel(tc, theta, basis_mu, basis_sigma, Bv, out):
         nc.sync.dma_start(out=bm[:], in_=basis_mu.rearrange("(c p t) -> p c t", p=P, t=PACK))
         raws = []
         for c in range(PASSES):
-            raw = llp.tile([P, PACK, D], BF16, tag="ll", align_bytes=64)
+            raw = logs.tile([P, PACK, D], BF16, tag="ll", align_bytes=64)
             nc.sync.dma_start(
                 out=raw[:],
                 in_=Bv[c * P * PACK : (c + 1) * P * PACK, :].rearrange("(p t) w -> p t w", t=PACK),
@@ -187,7 +170,7 @@ def tile_longtermattention_kernel(tc, theta, basis_mu, basis_sigma, Bv, out):
             if kind == "BR" or kind == "BM":
                 h = st[1]
                 src = rec if kind == "BR" else mu
-                bk = bps.tile([P, BANK], F32, tag=kind)
+                bk = spread.tile([P, BANK], F32, tag=kind)
                 for a in range(CHUNK_TILES):
                     i = h * CHUNK_TILES + a
                     nc.tensor.matmul(
@@ -203,7 +186,7 @@ def tile_longtermattention_kernel(tc, theta, basis_mu, basis_sigma, Bv, out):
                     mub[h] = bk
             elif kind == "LN":
                 u = st[1]
-                lt = llp.tile([P, PACK, CHUNK], F32, tag="ll", align_bytes=64)
+                lt = logs.tile([P, PACK, CHUNK], F32, tag="ll", align_bytes=64)
                 for t in range(PACK):
                     k = (u % 2) * PACK + t
                     nc.scalar.activation(
@@ -216,7 +199,7 @@ def tile_longtermattention_kernel(tc, theta, basis_mu, basis_sigma, Bv, out):
                 ll[u] = lt
             elif kind == "W":
                 u = st[1]
-                wt = wwp.tile([P, PACK, CHUNK], F32, tag="ww", align_bytes=64)
+                wt = work.tile([P, PACK, CHUNK], F32, tag="ww", align_bytes=64)
                 nc.scalar.activation(
                     out=wt[:].rearrange("p t n -> p (t n)"),
                     in_=ll[u][:].rearrange("p t n -> p (t n)"),
@@ -248,7 +231,7 @@ def tile_longtermattention_kernel(tc, theta, basis_mu, basis_sigma, Bv, out):
                 u = st[1]
                 cols = slice(st[2] * P, st[3] * P)
                 if u not in rb:
-                    rbt = rbp.tile([P, CHUNK, PACK], BF16, align_bytes=64)
+                    rbt = rows.tile([P, CHUNK, PACK], BF16, align_bytes=64)
                     rb[u] = rbt
                 nc.scalar.activation(
                     out=rb[u][:, cols, :].rearrange("p (m i) t -> p m t i", i=4),
@@ -260,8 +243,8 @@ def tile_longtermattention_kernel(tc, theta, basis_mu, basis_sigma, Bv, out):
                 u = st[1]
                 cols = slice(st[2] * P, st[3] * P)
                 if u not in cod:
-                    cdt = qp.tile([P, CHUNK], U32, align_bytes=64)
-                    sct = qp.tile([P, CHUNK], U8, align_bytes=64)
+                    cdt = packed.tile([P, CHUNK], U32, align_bytes=64)
+                    sct = packed.tile([P, CHUNK], U8, align_bytes=64)
                     cod[u], scl[u] = cdt, sct
                 nc.vector.quantize_mx(
                     out=cod[u][:, cols].bitcast(FP8X4),
@@ -270,7 +253,7 @@ def tile_longtermattention_kernel(tc, theta, basis_mu, basis_sigma, Bv, out):
                 )
             elif kind == "BVG":
                 c = st[1]
-                gt = wwp.tile([P, D, PACK], BF16, tag="ww", align_bytes=64)
+                gt = work.tile([P, D, PACK], BF16, tag="ww", align_bytes=64)
                 nc.vector.tensor_copy(
                     out=gt[:].rearrange("p (m i) t -> p m t i", i=4),
                     in_=raws[c][:].rearrange("p t (m i) -> p m t i", i=4),
@@ -287,7 +270,7 @@ def tile_longtermattention_kernel(tc, theta, basis_mu, basis_sigma, Bv, out):
                 h, a = st[1], st[2]
                 cols = slice(a * P, (a + 1) * P)
                 for dh in range(D // BANK):
-                    at = aps.tile([P, BANK], F32, tag="acc")
+                    at = sums.tile([P, BANK], F32, tag="acc")
                     dcols = slice(dh * BANK, (dh + 1) * BANK)
                     for c in range(PASSES):
                         nc.tensor.matmul_mx(
@@ -303,7 +286,7 @@ def tile_longtermattention_kernel(tc, theta, basis_mu, basis_sigma, Bv, out):
             elif kind == "EV":
                 h, a, dh, eng = st[1], st[2], st[3], st[4]
                 if (h, a // 2) not in ost:
-                    ot = op.tile([P, 2, D], F32)
+                    ot = results.tile([P, 2, D], F32)
                     ost[(h, a // 2)] = ot
                 dst = ost[(h, a // 2)][:, a % 2, dh * BANK : (dh + 1) * BANK]
                 if eng == "act":
@@ -311,6 +294,8 @@ def tile_longtermattention_kernel(tc, theta, basis_mu, basis_sigma, Bv, out):
                 else:
                     nc.vector.tensor_copy(out=dst, in_=acc[(h, a, dh)][:])
             elif kind == "ST":
-                h, half = st[1], st[2]
-                i0 = h * CHUNK_TILES + 2 * half
-                nc.sync.dma_start(out=out_v[:, i0 : i0 + 2, :], in_=ost[(h, half)][:])
+                h, a0, a1 = st[1], st[2], st[3]
+                i0 = h * CHUNK_TILES
+                nc.sync.dma_start(
+                    out=out_v[:, i0 + a0 : i0 + a1, :], in_=ost[(h, a0 // 2)][:, a0 % 2 : a0 % 2 + a1 - a0, :]
+                )

@@ -27,84 +27,131 @@ GROUPS = UNITS // GROUP
 
 FLOPS = 2 * ROWS * NB * D
 
-VECTOR_BANKS_A_UNIT = 4
-SCALAR_BANKS_A_UNIT = 2
-SCALAR_BANKS_BEFORE_THE_END = 6
+D2_FROM = 8
+H0 = D2_FROM // 2
+Z_ON_DVE = ()
 LAST_UNIT = UNITS - 1
+STEP_EV = (4, 4, 4)
+LAST_EV = (0, 2, 4, 6)
+TAIL_EV = (2, 2, 1, 0)
 
 
 def plan():
     steps = []
-    banks = []
-    emptied = [0]
-    copied = {}
+    pending = []
+    taken = [0]
+    done = {}
+    issued = {}
+    mxq = []
+    mxt = [0]
 
-    def empty(count, engine):
-        for s in range(min(count, len(banks) - emptied[0])):
-            h, a, half = banks[emptied[0]]
-            emptied[0] += 1
-            steps.append(("EV", h, a, half, engine))
+    def drain(n, eng):
+        for s in range(n):
+            if taken[0] >= len(pending):
+                return
+            h, a, dh = pending[taken[0]]
+            taken[0] += 1
+            steps.append(("EV", h, a, dh, eng))
             tiles = 1 if h == CHUNKS - 1 else 2
             first = a - a % tiles
-            copied[(h, first)] = copied.get((h, first), 0) + 1
-            if copied[(h, first)] == 2 * tiles:
+            done[(h, first)] = done.get((h, first), 0) + 1
+            if done[(h, first)] == 2 * tiles:
                 steps.append(("ST", h, first, first + tiles))
 
-    def passes(h, a):
-        steps.append(("MX", h, a))
-        banks.append((h, a, 0))
-        banks.append((h, a, 1))
+    def once(step):
+        if step not in issued:
+            issued[step] = 1
+            steps.append(step)
 
-    def logarithms(group):
-        for u in range(group * GROUP, (group + 1) * GROUP):
+    def bcast(kind, h):
+        if h < CHUNKS:
+            once((kind, h))
+
+    def squares(u, planes):
+        if D2_FROM <= u < UNITS:
+            for t in planes:
+                once(("D2", u, t))
+
+    def passes():
+        while mxt[0] < len(mxq) and len(pending) - taken[0] <= 2:
+            h, a = mxq[mxt[0]]
+            mxt[0] += 1
+            steps.append(("MX", h, a))
+            pending.append((h, a, 0))
+            pending.append((h, a, 1))
+
+    def empty(n, eng):
+        for s in range((n + 3) // 4):
+            drain(min(4, n - 4 * s), eng)
+            passes()
+
+    def logs(lo, hi):
+        for u in range(lo, hi):
+            bcast("BR", u // 2)
             steps.append(("LN", u))
-            if u % 2 == 1 and u // 2 + 2 < CHUNKS:
-                steps.append(("BR", u // 2 + 2))
+            if u % 2 == 1:
+                bcast("BR", u // 2 + 2)
 
-    for h in range(2):
-        steps.append(("BR", h))
-    for h in range(2):
-        steps.append(("BM", h))
-    for c in range(PASSES):
-        steps.append(("BVG", c))
-    for c in range(PASSES):
-        steps.append(("BVQ", c))
-    logarithms(0)
-    for group in range(GROUPS):
-        for u in range(group * GROUP, (group + 1) * GROUP):
-            before = u - GROUP
+    def quant(u, a0, a1):
+        steps.append(("Q", u, a0, a1))
+        if u % 2 == 1:
+            for a in range(a0, a1):
+                mxq.append((u // 2, a))
+
+    bcast("BR", 0)
+    bcast("BR", 1)
+    bcast("BM", 0)
+    bcast("BM", 1)
+    steps.append(("PREP",))
+    steps.append(("BVG", 0))
+    steps.append(("BVG", 1))
+    steps.append(("BVQ", 0))
+    steps.append(("BVQ", 1))
+    logs(0, GROUP)
+    for gi in range(GROUPS):
+        lo, hi = gi * GROUP, (gi + 1) * GROUP
+        last = gi + 1 == GROUPS
+        for idx in range(GROUP):
+            u = lo + idx
+            p = u - GROUP if gi > 0 else None
             steps.append(("W", u))
-            if group > 0:
-                steps.append(("F", before, 0, CHUNK_TILES))
-            steps.append(("A1", u))
-            steps.append(("B2", u))
-            if u % 2 == 1 and u // 2 + 2 < CHUNKS:
-                steps.append(("BM", u // 2 + 2))
-            if group == GROUPS - 1:
-                empty(SCALAR_BANKS_A_UNIT, "act")
-            if group > 0:
-                steps.append(("Q", before, 0, CHUNK_TILES))
-            steps.append(("Z", u, "dve" if u == LAST_UNIT else "pool"))
-            if group < GROUPS - 1:
-                empty(VECTOR_BANKS_A_UNIT, "dve")
-            if group > 0 and before % 2 == 1:
-                for a in range(CHUNK_TILES):
-                    passes(before // 2, a)
-        if group < GROUPS - 1:
-            logarithms(group + 1)
-    empty(SCALAR_BANKS_BEFORE_THE_END, "act")
+            if p is not None:
+                steps.append(("F", p, 0, CHUNK_TILES))
+            if u < D2_FROM:
+                steps.append(("A1", u))
+                steps.append(("B2", u))
+                if u % 2 == 1 and 2 * (u // 2 + 2) < D2_FROM:
+                    bcast("BM", u // 2 + 2)
+            else:
+                squares(u, (0, 1))
+                steps.append(("BDV", u, 0))
+                squares(u, (2,))
+                steps.append(("BDV", u, 1))
+                squares(u, (3,))
+                steps.append(("BDV", u, 2))
+                steps.append(("BDV", u, 3))
+            squares(u + 1, (0, 1))
+            if p is not None:
+                quant(p, 0, CHUNK_TILES)
+            steps.append(("Z", u, "dve" if u in Z_ON_DVE else "pool"))
+            empty(LAST_EV[idx] if last else STEP_EV[gi], "dve")
+        if not last:
+            logs(hi, hi + GROUP)
+            empty(16, "dve")
     for u in range(UNITS - GROUP, UNITS):
         width = 1 if u == LAST_UNIT else CHUNK_TILES
         for a0 in range(0, CHUNK_TILES, width):
             steps.append(("F", u, a0, a0 + width))
-            empty(width, "dve")
-            steps.append(("Q", u, a0, a0 + width))
-            if u % 2 == 1:
-                for a in range(a0, a0 + width):
-                    passes(u // 2, a)
-    while emptied[0] < len(banks):
-        empty(1, "act")
-        empty(1, "dve")
+    for u in range(UNITS - GROUP, UNITS):
+        width = 1 if u == LAST_UNIT else CHUNK_TILES
+        for a0 in range(0, CHUNK_TILES, width):
+            quant(u, a0, a0 + width)
+            passes()
+            empty(TAIL_EV[u - (UNITS - GROUP)], "dve")
+    while taken[0] < len(pending) or mxt[0] < len(mxq):
+        passes()
+        drain(1, "act")
+        drain(1, "dve")
     return steps
 
 
@@ -129,6 +176,8 @@ def tile_longtermattention_kernel(tc, theta, basis_mu, basis_sigma, Bv, out):
         nc.sync.dma_start(out=bs[:], in_=basis_sigma.rearrange("(c p t) -> p c t", p=P, t=PACK))
         bm = const.tile([P, PASSES, PACK], BF16)
         nc.sync.dma_start(out=bm[:], in_=basis_mu.rearrange("(c p t) -> p c t", p=P, t=PACK))
+        tmpb = const.tile([P, NB], BF16)
+        nc.sync.dma_start(out=tmpb[32:64, :], in_=basis_mu.partition_broadcast(32))
         raws = []
         for c in range(PASSES):
             raw = logs.tile([P, PACK, D], BF16, tag="ll", align_bytes=64)
@@ -164,6 +213,52 @@ def tile_longtermattention_kernel(tc, theta, basis_mu, basis_sigma, Bv, out):
         bvs = const.tile([P, PASSES, D], U8, align_bytes=64)
 
         recb, mub, ll, ww, rb, cod, scl, acc, ost, grp = {}, {}, {}, {}, {}, {}, {}, {}, {}, {}
+        d2 = {}
+        cj = const.tile([P, PASSES * PACK], F32)
+        lta = const.tile([P, CHUNK_TILES, NB], BF16)
+        rowsT = const.tile([P, CHUNKS - H0, P], BF16)
+
+        def prepare_squares():
+            nc.vector.tensor_tensor(out=cj[:], in0=bmf[:], in1=bmf[:], op=ALU.mult)
+            xq = const.tile([P, 2, TILES], F32)
+            nc.vector.tensor_tensor(out=xq[:, 0, :], in0=mu[:], in1=mu[:], op=ALU.mult)
+            nc.vector.tensor_scalar_mul(out=xq[:, 1, :], in0=mu[:], scalar1=-2.0 * kappa)
+            sq = const.tile([P, CHUNKS - H0, P], F32)
+            nc.vector.memset(sq[:], 0.0)
+            rest = xq
+            for e in range(3):
+                pc = const.tile([P, 2, TILES], BF16, name="pc%d" % e)
+                nc.vector.tensor_copy(out=pc[:], in_=rest[:])
+                nc.vector.tensor_copy(
+                    out=sq[:].rearrange("p h (g z) -> p h g z", z=32)[:, :, 0:2, 4 * e : 4 * e + 4],
+                    in_=pc[:, :, H0 * CHUNK_TILES :].rearrange("p g (h a) -> p h g a", a=CHUNK_TILES),
+                )
+                if e < 2:
+                    nxt = const.tile([P, 2, TILES], F32, name="rest%d" % e)
+                    nc.vector.tensor_tensor(out=nxt[:], in0=rest[:], in1=pc[:], op=ALU.subtract)
+                    rest = nxt
+            tp = sums.tile([P, BANK], F32, tag="acc")
+            for hh in range(CHUNKS - H0):
+                nc.tensor.transpose(tp[:, hh * P : (hh + 1) * P], sq[:, hh, :], ident[:])
+            nc.vector.tensor_copy(out=rowsT[:].rearrange("r h p -> r (h p)"), in_=tp[:])
+            gf = const.tile([P, NB], BF16)
+            nc.vector.memset(gf[:], 0.0)
+            nc.vector.memset(gf[0:32, :], 1.0)
+            nc.vector.tensor_copy(
+                out=gf[32:64, :].rearrange("r (c t m) -> r c t m", c=PASSES, t=PACK),
+                in_=tmpb[32:64, :].rearrange("r (c m t) -> r c t m", c=PASSES, t=PACK),
+            )
+            mask = const.tile([P, CHUNK_TILES], F32)
+            nc.vector.tensor_reduce(
+                out=mask[:],
+                in_=ident[:]
+                .rearrange("r (g z) -> r g z", z=32)[:, 0:2, 0:12]
+                .rearrange("r g (e a) -> r a g e", a=CHUNK_TILES),
+                axis=mybir.AxisListType.XY,
+                op=ALU.add,
+            )
+            for a in range(CHUNK_TILES):
+                nc.vector.tensor_scalar_mul(out=lta[:, a, :], in0=gf[:], scalar1=mask[:, a : a + 1])
 
         for st in plan():
             kind = st[0]
@@ -219,6 +314,32 @@ def tile_longtermattention_kernel(tc, theta, basis_mu, basis_sigma, Bv, out):
                         op0=ALU.subtract,
                         op1=ALU.mult,
                     )
+            elif kind == "PREP":
+                prepare_squares()
+            elif kind == "D2":
+                u, t = st[1], st[2]
+                k = (u % 2) * PACK + t
+                d2t = spread.tile([P, BANK], F32, tag="BM")
+                for a in range(CHUNK_TILES):
+                    nc.tensor.matmul(
+                        out=d2t[:, a * P : (a + 1) * P],
+                        lhsT=lta[:, a, k * P : (k + 1) * P],
+                        rhs=rowsT[:, u // 2 - H0, :],
+                        start=True,
+                        stop=True,
+                    )
+                d2[(u, t)] = d2t
+            elif kind == "BDV":
+                u, t = st[1], st[2]
+                k = (u % 2) * PACK + t
+                nc.vector.scalar_tensor_tensor(
+                    out=ww[u][:, t, :],
+                    in0=d2[(u, t)][:],
+                    scalar=cj[:, k : k + 1],
+                    in1=ww[u][:, t, :],
+                    op0=ALU.add,
+                    op1=ALU.mult,
+                )
             elif kind == "Z":
                 u = st[1]
                 wf = ww[u][:].rearrange("p t n -> p (t n)")

@@ -27,8 +27,14 @@ GROUPS = UNITS // GROUP
 
 FLOPS = 2 * ROWS * NB * D
 
-D2_FROM = 8
+D2_FROM = 4
 H0 = D2_FROM // 2
+PAIRED = (3, 5, 7)
+PLANES = PASSES * PACK
+TERMS = 7
+COMBOS = ((0, 0), (1, 0), (2, 0), (0, 1), (1, 1), (0, 2))
+SLOT = 8
+HOLD = True
 Z_ON_DVE = ()
 LAST_UNIT = UNITS - 1
 STEP_EV = (4, 4, 4)
@@ -89,6 +95,8 @@ def plan():
         for u in range(lo, hi):
             bcast("BR", u // 2)
             steps.append(("LN", u))
+            if u // 2 in PAIRED:
+                steps.append(("S", u))
             if u % 2 == 1:
                 bcast("BR", u // 2 + 2)
 
@@ -133,6 +141,8 @@ def plan():
             squares(u + 1, (0, 1))
             if p is not None:
                 quant(p, 0, CHUNK_TILES)
+                if HOLD:
+                    steps.append(("H", p))
             steps.append(("Z", u, "dve" if u in Z_ON_DVE else "pool"))
             empty(LAST_EV[idx] if last else STEP_EV[gi], "dve")
         if not last:
@@ -164,6 +174,7 @@ def tile_longtermattention_kernel(tc, theta, basis_mu, basis_sigma, Bv, out):
         const = ctx.enter_context(tc.tile_pool(name="const", bufs=1))
         logs = ctx.enter_context(tc.tile_pool(name="logs", bufs=8))
         work = ctx.enter_context(tc.tile_pool(name="work", bufs=6))
+        pair = ctx.enter_context(tc.tile_pool(name="pair", bufs=3))
         rows = ctx.enter_context(tc.tile_pool(name="rows", bufs=3))
         packed = ctx.enter_context(tc.tile_pool(name="packed", bufs=6))
         results = ctx.enter_context(tc.tile_pool(name="results", bufs=4))
@@ -176,8 +187,6 @@ def tile_longtermattention_kernel(tc, theta, basis_mu, basis_sigma, Bv, out):
         nc.sync.dma_start(out=bs[:], in_=basis_sigma.rearrange("(c p t) -> p c t", p=P, t=PACK))
         bm = const.tile([P, PASSES, PACK], BF16)
         nc.sync.dma_start(out=bm[:], in_=basis_mu.rearrange("(c p t) -> p c t", p=P, t=PACK))
-        tmpb = const.tile([P, NB], BF16)
-        nc.sync.dma_start(out=tmpb[32:64, :], in_=basis_mu.partition_broadcast(32))
         raws = []
         for c in range(PASSES):
             raw = logs.tile([P, PACK, D], BF16, tag="ll", align_bytes=64)
@@ -189,11 +198,17 @@ def tile_longtermattention_kernel(tc, theta, basis_mu, basis_sigma, Bv, out):
 
         ident = const.tile([P, P], F32)
         make_identity(nc, ident[:])
+        identb = const.tile([P, P], BF16)
+        make_identity(nc, identb[:])
+        rowq = const.tile([P, TILES, P], BF16)
+        nc.gpsimd.memset(rowq[:], 0.0)
 
         warm = const.tile([P, 1], F32)
         nc.vector.memset(warm[:], 1.0)
         warm2 = const.tile([P, 1], F32)
         nc.scalar.activation(out=warm2[:], in_=warm[:], func=AF.Ln)
+        cofq = const.tile([P, 2 * PLANES, P], BF16)
+        nc.vector.memset(cofq[:], 0.0)
 
         rec = const.tile([P, TILES], F32)
         nc.vector.reciprocal(out=rec[:], in_=th[:, :, 1])
@@ -213,52 +228,87 @@ def tile_longtermattention_kernel(tc, theta, basis_mu, basis_sigma, Bv, out):
         bvs = const.tile([P, PASSES, D], U8, align_bytes=64)
 
         recb, mub, ll, ww, rb, cod, scl, acc, ost, grp = {}, {}, {}, {}, {}, {}, {}, {}, {}, {}
-        d2 = {}
-        cj = const.tile([P, PASSES * PACK], F32)
-        lta = const.tile([P, CHUNK_TILES, NB], BF16)
-        rowsT = const.tile([P, CHUNKS - H0, P], BF16)
+        d2, ss = {}, {}
+        pi2 = math.pi * math.pi
+        bmv = bm[:].rearrange("p c t -> p (c t)")
+        rowsT = const.tile([P, (CHUNKS - H0) * CHUNK_TILES, P], BF16)
+        cofT = const.tile([P, 2 * PLANES, P], BF16)
+        kc = const.tile([P, 2 * PLANES], F32)
 
-        def prepare_squares():
-            nc.vector.tensor_tensor(out=cj[:], in0=bmf[:], in1=bmf[:], op=ALU.mult)
-            xq = const.tile([P, 2, TILES], F32)
-            nc.vector.tensor_tensor(out=xq[:, 0, :], in0=mu[:], in1=mu[:], op=ALU.mult)
-            nc.vector.tensor_scalar_mul(out=xq[:, 1, :], in0=mu[:], scalar1=-2.0 * kappa)
-            sq = const.tile([P, CHUNKS - H0, P], F32)
-            nc.vector.memset(sq[:], 0.0)
-            rest = xq
+        def split3(src, shape, name):
+            pieces = []
+            rest = src
             for e in range(3):
-                pc = const.tile([P, 2, TILES], BF16, name="pc%d" % e)
+                pc = const.tile(shape, BF16, name="%s_p%d" % (name, e))
                 nc.vector.tensor_copy(out=pc[:], in_=rest[:])
-                nc.vector.tensor_copy(
-                    out=sq[:].rearrange("p h (g z) -> p h g z", z=32)[:, :, 0:2, 4 * e : 4 * e + 4],
-                    in_=pc[:, :, H0 * CHUNK_TILES :].rearrange("p g (h a) -> p h g a", a=CHUNK_TILES),
-                )
+                pieces.append(pc)
                 if e < 2:
-                    nxt = const.tile([P, 2, TILES], F32, name="rest%d" % e)
+                    nxt = const.tile(shape, F32, name="%s_r%d" % (name, e))
                     nc.vector.tensor_tensor(out=nxt[:], in0=rest[:], in1=pc[:], op=ALU.subtract)
                     rest = nxt
-            tp = sums.tile([P, BANK], F32, tag="acc")
+            return pieces
+
+        def prepare_rows():
+            xf = const.tile([P, TERMS, TILES], F32)
+            sg = const.tile([P, TILES], F32)
+            nc.vector.tensor_scalar_mul(out=sg[:], in0=rec[:], scalar1=-0.5)
+            nc.vector.tensor_scalar_mul(out=xf[:, 4, :], in0=rec[:], scalar1=-2.0 * pi2)
+            nc.vector.scalar_tensor_tensor(
+                out=xf[:, 3, :], in0=rec[:], scalar=4.0 * pi2, in1=th[:, :, 0], op0=ALU.mult, op1=ALU.mult
+            )
+            nc.vector.scalar_tensor_tensor(
+                out=xf[:, 1, :], in0=xf[:, 3, :], scalar=1.0 / (16.0 * pi2), in1=xf[:, 3, :], op0=ALU.mult, op1=ALU.mult
+            )
+            nc.vector.tensor_tensor(out=xf[:, 0, :], in0=xf[:, 1, :], in1=sg[:], op=ALU.mult)
+            nc.vector.tensor_tensor(out=xf[:, 2, :], in0=xf[:, 3, :], in1=sg[:], op=ALU.mult)
+            nc.vector.tensor_scalar_mul(out=xf[:, 5, :], in0=xf[:, 1, :], scalar1=0.5 / math.pi)
+            nc.vector.tensor_scalar_mul(out=xf[:, 6, :], in0=xf[:, 3, :], scalar1=0.5 / math.pi)
+            pcs = split3(xf, [P, TERMS, TILES], "xf")
+            for blk, (e, f) in enumerate(COMBOS):
+                nc.vector.tensor_copy(
+                    out=rowq[:, :, blk * SLOT : blk * SLOT + TERMS], in_=pcs[e][:].rearrange("p f i -> p i f")
+                )
+
+        def prepare_coefficients():
+            cf = const.tile([P, TERMS, 2 * PLANES], F32)
+            nc.vector.memset(cf[:], 0.0)
+            lo = slice(0, PLANES)
+            hi = slice(PLANES, 2 * PLANES)
+            gg = const.tile([P, PLANES], F32)
+            nc.vector.tensor_tensor(out=gg[:], in0=bsf, in1=bsf, op=ALU.mult)
+            nc.vector.memset(cf[:, 0, lo], 1.0)
+            nc.vector.memset(cf[:, 5, hi], 1.0)
+            nc.vector.tensor_copy(out=cf[:, 6, hi], in_=bmv)
+            nc.vector.tensor_tensor(out=kc[:, hi], in0=bmf[:], in1=bmf[:], op=ALU.mult)
+            cfp = cf[:, 1, lo].rearrange("p (q two) -> p q two", two=2)
+            ggp = gg[:].rearrange("p (q two) -> p q two", two=2)
+            nc.vector.tensor_copy(out=cfp[:, :, 0], in_=ggp[:, :, 1])
+            nc.vector.tensor_copy(out=cfp[:, :, 1], in_=ggp[:, :, 0])
+            nc.vector.tensor_copy(out=cf[:, 2, lo], in_=bmv)
+            nc.vector.tensor_tensor(out=cf[:, 3, lo], in0=cf[:, 2, lo], in1=cf[:, 1, lo], op=ALU.mult)
+            nc.vector.tensor_tensor(out=cf[:, 4, lo], in0=cf[:, 2, lo], in1=cf[:, 2, lo], op=ALU.mult)
+            nc.vector.scalar_tensor_tensor(
+                out=kc[:, lo], in0=cf[:, 4, lo], scalar=4.0 * pi2, in1=cf[:, 1, lo], op0=ALU.mult, op1=ALU.mult
+            )
+            pcs = split3(cf, [P, TERMS, 2 * PLANES], "cf")
+            for blk, (e, f) in enumerate(COMBOS):
+                nc.vector.tensor_copy(
+                    out=cofq[:, :, blk * SLOT : blk * SLOT + TERMS], in_=pcs[f][:].rearrange("p f k -> p k f")
+                )
+
+        def turn(dst, d0, src, s0):
+            tp = sums.tile([P, 4, P], BF16, tag="acc")
+            for j in range(4):
+                nc.tensor.transpose(tp[:, j, :], src[:, s0 + j, :], identb[:])
+            nc.vector.tensor_copy(out=dst[:, d0 : d0 + 4, :], in_=tp[:])
+
+        def prepare_squares():
+            prepare_coefficients()
+            prepare_rows()
+            for j0 in range(0, 2 * PLANES, 4):
+                turn(cofT, j0, cofq, j0)
             for hh in range(CHUNKS - H0):
-                nc.tensor.transpose(tp[:, hh * P : (hh + 1) * P], sq[:, hh, :], ident[:])
-            nc.vector.tensor_copy(out=rowsT[:].rearrange("r h p -> r (h p)"), in_=tp[:])
-            gf = const.tile([P, NB], BF16)
-            nc.vector.memset(gf[:], 0.0)
-            nc.vector.memset(gf[0:32, :], 1.0)
-            nc.vector.tensor_copy(
-                out=gf[32:64, :].rearrange("r (c t m) -> r c t m", c=PASSES, t=PACK),
-                in_=tmpb[32:64, :].rearrange("r (c m t) -> r c t m", c=PASSES, t=PACK),
-            )
-            mask = const.tile([P, CHUNK_TILES], F32)
-            nc.vector.tensor_reduce(
-                out=mask[:],
-                in_=ident[:]
-                .rearrange("r (g z) -> r g z", z=32)[:, 0:2, 0:12]
-                .rearrange("r g (e a) -> r a g e", a=CHUNK_TILES),
-                axis=mybir.AxisListType.XY,
-                op=ALU.add,
-            )
-            for a in range(CHUNK_TILES):
-                nc.vector.tensor_scalar_mul(out=lta[:, a, :], in0=gf[:], scalar1=mask[:, a : a + 1])
+                turn(rowsT, hh * CHUNK_TILES, rowq, (H0 + hh) * CHUNK_TILES)
 
         for st in plan():
             kind = st[0]
@@ -268,13 +318,7 @@ def tile_longtermattention_kernel(tc, theta, basis_mu, basis_sigma, Bv, out):
                 bk = spread.tile([P, BANK], F32, tag=kind)
                 for a in range(CHUNK_TILES):
                     i = h * CHUNK_TILES + a
-                    nc.tensor.matmul(
-                        out=bk[:, a * P : (a + 1) * P],
-                        lhsT=src[:, i : i + 1].to_broadcast([P, P]),
-                        rhs=ident[:],
-                        start=True,
-                        stop=True,
-                    )
+                    nc.tensor.transpose(bk[:, a * P : (a + 1) * P], src[:, i : i + 1].to_broadcast([P, P]), ident[:])
                 if kind == "BR":
                     recb[h] = bk
                 else:
@@ -292,16 +336,26 @@ def tile_longtermattention_kernel(tc, theta, basis_mu, basis_sigma, Bv, out):
                         scale=-math.pi,
                     )
                 ll[u] = lt
+            elif kind == "S":
+                u = st[1]
+                sst = pair.tile([P, PACK // 2, CHUNK], F32)
+                lv = ll[u][:].rearrange("p (q two) n -> p q two n", two=2)
+                nc.gpsimd.tensor_tensor(out=sst[:], in0=lv[:, :, 0, :], in1=lv[:, :, 1, :], op=ALU.add)
+                ss[u] = sst
             elif kind == "W":
                 u = st[1]
                 wt = work.tile([P, PACK, CHUNK], F32, tag="ww", align_bytes=64)
-                nc.scalar.activation(
-                    out=wt[:].rearrange("p t n -> p (t n)"),
-                    in_=ll[u][:].rearrange("p t n -> p (t n)"),
-                    func=AF.Exp,
-                    scale=-1.0,
-                )
                 ww[u] = wt
+                if u // 2 in PAIRED:
+                    sf = ss[u][:].rearrange("p q n -> p (q n)")
+                    nc.scalar.activation(out=sf, in_=sf, func=AF.Exp, scale=-1.0)
+                else:
+                    nc.scalar.activation(
+                        out=wt[:].rearrange("p t n -> p (t n)"),
+                        in_=ll[u][:].rearrange("p t n -> p (t n)"),
+                        func=AF.Exp,
+                        scale=-1.0,
+                    )
             elif kind == "A1" or kind == "B2":
                 u = st[1]
                 for t in range(PACK):
@@ -320,26 +374,30 @@ def tile_longtermattention_kernel(tc, theta, basis_mu, basis_sigma, Bv, out):
                 u, t = st[1], st[2]
                 k = (u % 2) * PACK + t
                 d2t = spread.tile([P, BANK], F32, tag="BM")
-                for a in range(CHUNK_TILES):
-                    nc.tensor.matmul(
-                        out=d2t[:, a * P : (a + 1) * P],
-                        lhsT=lta[:, a, k * P : (k + 1) * P],
-                        rhs=rowsT[:, u // 2 - H0, :],
-                        start=True,
-                        stop=True,
-                    )
+                n0 = (u // 2 - H0) * CHUNK_TILES
+                nc.tensor.matmul(
+                    out=d2t[:],
+                    lhsT=cofT[:, k if u // 2 in PAIRED else PLANES + k, :],
+                    rhs=rowsT[:, n0 : n0 + CHUNK_TILES, :].rearrange("r a p -> r (a p)"),
+                    start=True,
+                    stop=True,
+                )
                 d2[(u, t)] = d2t
             elif kind == "BDV":
                 u, t = st[1], st[2]
                 k = (u % 2) * PACK + t
+                kk = k if u // 2 in PAIRED else PLANES + k
                 nc.vector.scalar_tensor_tensor(
                     out=ww[u][:, t, :],
                     in0=d2[(u, t)][:],
-                    scalar=cj[:, k : k + 1],
-                    in1=ww[u][:, t, :],
+                    scalar=kc[:, kk : kk + 1],
+                    in1=ss[u][:, t // 2, :] if u // 2 in PAIRED else ww[u][:, t, :],
                     op0=ALU.add,
                     op1=ALU.mult,
                 )
+            elif kind == "H":
+                jk = const.tile([P, 1], U32, name="junk")
+                nc.gpsimd.tensor_copy(out=jk[:], in_=cod[st[1]][:, 0:1])
             elif kind == "Z":
                 u = st[1]
                 wf = ww[u][:].rearrange("p t n -> p (t n)")

@@ -34,12 +34,16 @@ PLANES = PASSES * PACK
 TERMS = 7
 COMBOS = ((0, 0), (1, 0), (2, 0), (0, 1), (1, 1), (0, 2))
 SLOT = 8
-HOLD = True
-Z_ON_DVE = ()
+HOLD = False
+S_ON_DVE = ()
+Z_ON_DVE = (15,)
 LAST_UNIT = UNITS - 1
 STEP_EV = (4, 4, 4)
-LAST_EV = (0, 2, 4, 6)
-TAIL_EV = (2, 2, 1, 0)
+LAST_EV = (0, 2, 2, 0)
+TAIL_EV = (0, 1, 2, 1)
+LN_FROM_SBUF = False
+LAST_ACT = (0, 0, 1, 1)
+TAIL_ACT = (2, 2, 2, 1)
 
 
 def plan():
@@ -78,11 +82,14 @@ def plan():
             for t in planes:
                 once(("D2", u, t))
 
+    extra = [0]
+
     def passes():
-        while mxt[0] < len(mxq) and len(pending) - taken[0] <= 2:
+        while mxt[0] < len(mxq) and len(pending) - taken[0] <= 2 + 2 * extra[0]:
             h, a = mxq[mxt[0]]
             mxt[0] += 1
-            steps.append(("MX", h, a))
+            cyc = ("acc", "acc", "BR", "BM")[: 2 + extra[0]]
+            steps.append(("MX", h, a, cyc[mxt[0] % len(cyc)]))
             pending.append((h, a, 0))
             pending.append((h, a, 1))
 
@@ -122,9 +129,13 @@ def plan():
         for idx in range(GROUP):
             u = lo + idx
             p = u - GROUP if gi > 0 else None
+            if last and idx == 0:
+                extra[0] = 1
             steps.append(("W", u))
             if p is not None:
                 steps.append(("F", p, 0, CHUNK_TILES))
+            if last:
+                drain(LAST_ACT[idx], "act")
             if u < D2_FROM:
                 steps.append(("A1", u))
                 steps.append(("B2", u))
@@ -148,13 +159,12 @@ def plan():
         if not last:
             logs(hi, hi + GROUP)
             empty(16, "dve")
+    extra[0] = 2
     for u in range(UNITS - GROUP, UNITS):
         width = 1 if u == LAST_UNIT else CHUNK_TILES
         for a0 in range(0, CHUNK_TILES, width):
             steps.append(("F", u, a0, a0 + width))
-    for u in range(UNITS - GROUP, UNITS):
-        width = 1 if u == LAST_UNIT else CHUNK_TILES
-        for a0 in range(0, CHUNK_TILES, width):
+            drain(TAIL_ACT[u - (UNITS - GROUP)], "act")
             quant(u, a0, a0 + width)
             passes()
             empty(TAIL_EV[u - (UNITS - GROUP)], "dve")
@@ -175,6 +185,7 @@ def tile_longtermattention_kernel(tc, theta, basis_mu, basis_sigma, Bv, out):
         logs = ctx.enter_context(tc.tile_pool(name="logs", bufs=8))
         work = ctx.enter_context(tc.tile_pool(name="work", bufs=6))
         pair = ctx.enter_context(tc.tile_pool(name="pair", bufs=3))
+        flat = ctx.enter_context(tc.tile_pool(name="flat", bufs=3))
         rows = ctx.enter_context(tc.tile_pool(name="rows", bufs=3))
         packed = ctx.enter_context(tc.tile_pool(name="packed", bufs=6))
         results = ctx.enter_context(tc.tile_pool(name="results", bufs=4))
@@ -200,8 +211,6 @@ def tile_longtermattention_kernel(tc, theta, basis_mu, basis_sigma, Bv, out):
         make_identity(nc, ident[:])
         identb = const.tile([P, P], BF16)
         make_identity(nc, identb[:])
-        rowq = const.tile([P, TILES, P], BF16)
-        nc.gpsimd.memset(rowq[:], 0.0)
 
         warm = const.tile([P, 1], F32)
         nc.vector.memset(warm[:], 1.0)
@@ -223,6 +232,8 @@ def tile_longtermattention_kernel(tc, theta, basis_mu, basis_sigma, Bv, out):
         )
         bmf = const.tile([P, PASSES * PACK], F32)
         nc.vector.tensor_scalar_mul(out=bmf[:], in0=bm[:].rearrange("p c t -> p (c t)"), scalar1=kappa)
+        rowq = const.tile([P, TILES, P], BF16)
+        nc.vector.memset(rowq[:], 0.0)
 
         bvc = const.tile([P, PASSES, D], U32, align_bytes=64)
         bvs = const.tile([P, PASSES, D], U8, align_bytes=64)
@@ -319,7 +330,11 @@ def tile_longtermattention_kernel(tc, theta, basis_mu, basis_sigma, Bv, out):
                 for a in range(CHUNK_TILES):
                     i = h * CHUNK_TILES + a
                     nc.tensor.transpose(bk[:, a * P : (a + 1) * P], src[:, i : i + 1].to_broadcast([P, P]), ident[:])
-                if kind == "BR":
+                if kind == "BR" and LN_FROM_SBUF:
+                    rc = flat.tile([P, BANK], F32)
+                    nc.vector.tensor_copy(out=rc[:], in_=bk[:])
+                    recb[h] = rc
+                elif kind == "BR":
                     recb[h] = bk
                 else:
                     mub[h] = bk
@@ -340,7 +355,10 @@ def tile_longtermattention_kernel(tc, theta, basis_mu, basis_sigma, Bv, out):
                 u = st[1]
                 sst = pair.tile([P, PACK // 2, CHUNK], F32)
                 lv = ll[u][:].rearrange("p (q two) n -> p q two n", two=2)
-                nc.gpsimd.tensor_tensor(out=sst[:], in0=lv[:, :, 0, :], in1=lv[:, :, 1, :], op=ALU.add)
+                if u in S_ON_DVE:
+                    nc.vector.tensor_tensor(out=sst[:], in0=lv[:, :, 0, :], in1=lv[:, :, 1, :], op=ALU.add)
+                else:
+                    nc.gpsimd.tensor_tensor(out=sst[:], in0=lv[:, :, 0, :], in1=lv[:, :, 1, :], op=ALU.add)
                 ss[u] = sst
             elif kind == "W":
                 u = st[1]
@@ -449,7 +467,10 @@ def tile_longtermattention_kernel(tc, theta, basis_mu, basis_sigma, Bv, out):
                 h, a = st[1], st[2]
                 cols = slice(a * P, (a + 1) * P)
                 for dh in range(D // BANK):
-                    at = sums.tile([P, BANK], F32, tag="acc")
+                    if st[3] == "acc":
+                        at = sums.tile([P, BANK], F32, tag="acc")
+                    else:
+                        at = spread.tile([P, BANK], F32, tag=st[3])
                     dcols = slice(dh * BANK, (dh + 1) * BANK)
                     for c in range(PASSES):
                         nc.tensor.matmul_mx(

@@ -7,6 +7,7 @@ from concourse.masks import make_identity
 F32 = mybir.dt.float32
 BF16 = mybir.dt.bfloat16
 U32 = mybir.dt.uint32
+I32 = mybir.dt.int32
 U8 = mybir.dt.uint8
 FP8X4 = mybir.dt.float8_e4m3fn_x4
 AF = mybir.ActivationFunctionType
@@ -27,8 +28,9 @@ GROUPS = UNITS // GROUP
 
 FLOPS = 2 * ROWS * NB * D
 
-D2_FROM = 4
-H0 = D2_FROM // 2
+CLASSIC = (2, 4)
+FED = (0, 1, 3, 5, 6, 7)
+FED_RUNS = ((0, 2), (3, 4), (5, 8))
 PAIRED = (3, 5, 7)
 PLANES = PASSES * PACK
 TERMS = 7
@@ -78,9 +80,11 @@ def plan():
             once((kind, h))
 
     def squares(u, planes):
-        if D2_FROM <= u < UNITS:
+        if u < UNITS and u // 2 in FED:
             for t in planes:
                 once(("D2", u, t))
+        elif u < UNITS:
+            once(("BM", u // 2))
 
     extra = [0]
 
@@ -115,13 +119,10 @@ def plan():
 
     bcast("BR", 0)
     bcast("BR", 1)
-    bcast("BM", 0)
-    bcast("BM", 1)
-    steps.append(("PREP",))
+    steps.append(("PREP", 0))
+    squares(0, (0, 1))
     steps.append(("BVG", 0))
     steps.append(("BVG", 1))
-    steps.append(("BVQ", 0))
-    steps.append(("BVQ", 1))
     logs(0, GROUP)
     for gi in range(GROUPS):
         lo, hi = gi * GROUP, (gi + 1) * GROUP
@@ -136,11 +137,9 @@ def plan():
                 steps.append(("F", p, 0, CHUNK_TILES))
             if last:
                 drain(LAST_ACT[idx], "act")
-            if u < D2_FROM:
+            if u // 2 in CLASSIC:
                 steps.append(("A1", u))
                 steps.append(("B2", u))
-                if u % 2 == 1 and 2 * (u // 2 + 2) < D2_FROM:
-                    bcast("BM", u // 2 + 2)
             else:
                 squares(u, (0, 1))
                 steps.append(("BDV", u, 0))
@@ -156,6 +155,10 @@ def plan():
                     steps.append(("H", p))
             steps.append(("Z", u, "dve" if u in Z_ON_DVE else "pool"))
             empty(LAST_EV[idx] if last else STEP_EV[gi], "dve")
+        if gi == 0:
+            steps.append(("BVQ", 0))
+            steps.append(("BVQ", 1))
+            steps.append(("PREP", 1))
         if not last:
             logs(hi, hi + GROUP)
             empty(16, "dve")
@@ -217,7 +220,10 @@ def tile_longtermattention_kernel(tc, theta, basis_mu, basis_sigma, Bv, out):
         warm2 = const.tile([P, 1], F32)
         nc.scalar.activation(out=warm2[:], in_=warm[:], func=AF.Ln)
         cofq = const.tile([P, 2 * PLANES, P], BF16)
-        nc.vector.memset(cofq[:], 0.0)
+        nc.vector.memset(cofq[:].bitcast(I32), 0)
+        rowq = const.tile([P, TILES, P], BF16)
+        for h0, h1 in FED_RUNS:
+            nc.vector.memset(rowq[:, h0 * CHUNK_TILES : h1 * CHUNK_TILES, :].bitcast(I32), 0)
 
         rec = const.tile([P, TILES], F32)
         nc.vector.reciprocal(out=rec[:], in_=th[:, :, 1])
@@ -232,8 +238,6 @@ def tile_longtermattention_kernel(tc, theta, basis_mu, basis_sigma, Bv, out):
         )
         bmf = const.tile([P, PASSES * PACK], F32)
         nc.vector.tensor_scalar_mul(out=bmf[:], in0=bm[:].rearrange("p c t -> p (c t)"), scalar1=kappa)
-        rowq = const.tile([P, TILES, P], BF16)
-        nc.vector.memset(rowq[:], 0.0)
 
         bvc = const.tile([P, PASSES, D], U32, align_bytes=64)
         bvs = const.tile([P, PASSES, D], U8, align_bytes=64)
@@ -242,7 +246,7 @@ def tile_longtermattention_kernel(tc, theta, basis_mu, basis_sigma, Bv, out):
         d2, ss = {}, {}
         pi2 = math.pi * math.pi
         bmv = bm[:].rearrange("p c t -> p (c t)")
-        rowsT = const.tile([P, (CHUNKS - H0) * CHUNK_TILES, P], BF16)
+        rowsT = const.tile([P, len(FED) * CHUNK_TILES, P], BF16)
         cofT = const.tile([P, 2 * PLANES, P], BF16)
         kc = const.tile([P, 2 * PLANES], F32)
 
@@ -313,13 +317,16 @@ def tile_longtermattention_kernel(tc, theta, basis_mu, basis_sigma, Bv, out):
                 nc.tensor.transpose(tp[:, j, :], src[:, s0 + j, :], identb[:])
             nc.vector.tensor_copy(out=dst[:, d0 : d0 + 4, :], in_=tp[:])
 
-        def prepare_squares():
-            prepare_coefficients()
-            prepare_rows()
+        def prepare_squares(part):
+            if part == 0:
+                prepare_coefficients()
+                prepare_rows()
             for j0 in range(0, 2 * PLANES, 4):
-                turn(cofT, j0, cofq, j0)
-            for hh in range(CHUNKS - H0):
-                turn(rowsT, hh * CHUNK_TILES, rowq, (H0 + hh) * CHUNK_TILES)
+                if (j0 >= PLANES) == (part == 0):
+                    turn(cofT, j0, cofq, j0)
+            for hh in range(len(FED)):
+                if (FED[hh] < GROUP // 2) == (part == 0):
+                    turn(rowsT, hh * CHUNK_TILES, rowq, FED[hh] * CHUNK_TILES)
 
         for st in plan():
             kind = st[0]
@@ -387,12 +394,12 @@ def tile_longtermattention_kernel(tc, theta, basis_mu, basis_sigma, Bv, out):
                         op1=ALU.mult,
                     )
             elif kind == "PREP":
-                prepare_squares()
+                prepare_squares(st[1])
             elif kind == "D2":
                 u, t = st[1], st[2]
                 k = (u % 2) * PACK + t
                 d2t = spread.tile([P, BANK], F32, tag="BM")
-                n0 = (u // 2 - H0) * CHUNK_TILES
+                n0 = FED.index(u // 2) * CHUNK_TILES
                 nc.tensor.matmul(
                     out=d2t[:],
                     lhsT=cofT[:, k if u // 2 in PAIRED else PLANES + k, :],

import math
from contextlib import ExitStack

import concourse.mybir as mybir
from concourse.masks import make_identity

F32 = mybir.dt.float32
BF16 = mybir.dt.bfloat16
U32 = mybir.dt.uint32
I32 = mybir.dt.int32
U8 = mybir.dt.uint8
FP8X4 = mybir.dt.float8_e4m3fn_x4
AF = mybir.ActivationFunctionType
ALU = mybir.AluOpType

P = 128
ROWS, NB, D = 4096, 1024, 1024
PACK = 4
PASSES = NB // (P * PACK)
TILES = ROWS // P
CHUNK_TILES = 4
CHUNK = CHUNK_TILES * P
CHUNKS = TILES // CHUNK_TILES
UNITS = CHUNKS * PASSES
BANK = 512
GROUP = 4
GROUPS = UNITS // GROUP

FLOPS = 2 * ROWS * NB * D

CLASSIC = (2, 4)
FED = (0, 1, 3, 5, 6, 7)
FED_RUNS = ((0, 2), (3, 4), (5, 8))
PAIRED = (3, 5, 7)
PLANES = PASSES * PACK
TERMS = 7
COMBOS = ((0, 0), (1, 0), (2, 0), (0, 1), (1, 1), (0, 2))
SLOT = 8
HOLD = False
S_ON_DVE = ()
Z_ON_DVE = (15,)
LAST_UNIT = UNITS - 1
STEP_EV = (4, 4, 4)
LAST_EV = (0, 2, 2, 0)
TAIL_EV = (0, 1, 2, 1)
LN_FROM_SBUF = False
LAST_ACT = (0, 0, 1, 1)
TAIL_ACT = (2, 2, 2, 1)


def plan():
    steps = []
    pending = []
    taken = [0]
    done = {}
    issued = {}
    mxq = []
    mxt = [0]

    def drain(n, eng):
        for s in range(n):
            if taken[0] >= len(pending):
                return
            h, a, dh = pending[taken[0]]
            taken[0] += 1
            steps.append(("EV", h, a, dh, eng))
            tiles = 1 if h == CHUNKS - 1 else 2
            first = a - a % tiles
            done[(h, first)] = done.get((h, first), 0) + 1
            if done[(h, first)] == 2 * tiles:
                steps.append(("ST", h, first, first + tiles))

    def once(step):
        if step not in issued:
            issued[step] = 1
            steps.append(step)

    def bcast(kind, h):
        if h < CHUNKS:
            once((kind, h))

    def squares(u, planes):
        if u < UNITS and u // 2 in FED:
            for t in planes:
                once(("D2", u, t))
        elif u < UNITS:
            once(("BM", u // 2))

    extra = [0]

    def passes():
        while mxt[0] < len(mxq) and len(pending) - taken[0] <= 2 + 2 * extra[0]:
            h, a = mxq[mxt[0]]
            mxt[0] += 1
            cyc = ("acc", "acc", "BR", "BM")[: 2 + extra[0]]
            steps.append(("MX", h, a, cyc[mxt[0] % len(cyc)]))
            pending.append((h, a, 0))
            pending.append((h, a, 1))

    def empty(n, eng):
        for s in range((n + 3) // 4):
            drain(min(4, n - 4 * s), eng)
            passes()

    def logs(lo, hi):
        for u in range(lo, hi):
            bcast("BR", u // 2)
            steps.append(("LN", u))
            if u // 2 in PAIRED:
                steps.append(("S", u))
            if u % 2 == 1:
                bcast("BR", u // 2 + 2)

    def quant(u, a0, a1):
        steps.append(("Q", u, a0, a1))
        if u % 2 == 1:
            for a in range(a0, a1):
                mxq.append((u // 2, a))

    bcast("BR", 0)
    bcast("BR", 1)
    steps.append(("PREP", 0))
    squares(0, (0, 1))
    steps.append(("BVG", 0))
    steps.append(("BVG", 1))
    logs(0, GROUP)
    for gi in range(GROUPS):
        lo, hi = gi * GROUP, (gi + 1) * GROUP
        last = gi + 1 == GROUPS
        for idx in range(GROUP):
            u = lo + idx
            p = u - GROUP if gi > 0 else None
            if last and idx == 0:
                extra[0] = 1
            steps.append(("W", u))
            if p is not None:
                steps.append(("F", p, 0, CHUNK_TILES))
            if last:
                drain(LAST_ACT[idx], "act")
            if u // 2 in CLASSIC:
                steps.append(("A1", u))
                steps.append(("B2", u))
            else:
                squares(u, (0, 1))
                steps.append(("BDV", u, 0))
                squares(u, (2,))
                steps.append(("BDV", u, 1))
                squares(u, (3,))
                steps.append(("BDV", u, 2))
                steps.append(("BDV", u, 3))
            squares(u + 1, (0, 1))
            if p is not None:
                quant(p, 0, CHUNK_TILES)
                if HOLD:
                    steps.append(("H", p))
            steps.append(("Z", u, "dve" if u in Z_ON_DVE else "pool"))
            empty(LAST_EV[idx] if last else STEP_EV[gi], "dve")
        if gi == 0:
            steps.append(("BVQ", 0))
            steps.append(("BVQ", 1))
            steps.append(("PREP", 1))
        if not last:
            logs(hi, hi + GROUP)
            empty(16, "dve")
    extra[0] = 2
    for u in range(UNITS - GROUP, UNITS):
        width = 1 if u == LAST_UNIT else CHUNK_TILES
        for a0 in range(0, CHUNK_TILES, width):
            steps.append(("F", u, a0, a0 + width))
            drain(TAIL_ACT[u - (UNITS - GROUP)], "act")
            quant(u, a0, a0 + width)
            passes()
            empty(TAIL_EV[u - (UNITS - GROUP)], "dve")
    while taken[0] < len(pending) or mxt[0] < len(mxq):
        passes()
        drain(1, "act")
        drain(1, "dve")
    return steps


def tile_longtermattention_kernel(tc, theta, basis_mu, basis_sigma, Bv, out):
    nc = tc.nc
    out_v = out.rearrange("(p i) d -> p i d", i=TILES)
    kappa = math.sqrt(2.0 * math.pi)
    with ExitStack() as ctx:
        ctx.enter_context(tc.manual_schedule())
        const = ctx.enter_context(tc.tile_pool(name="const", bufs=1))
        logs = ctx.enter_context(tc.tile_pool(name="logs", bufs=8))
        work = ctx.enter_context(tc.tile_pool(name="work", bufs=6))
        pair = ctx.enter_context(tc.tile_pool(name="pair", bufs=3))
        flat = ctx.enter_context(tc.tile_pool(name="flat", bufs=3))
        rows = ctx.enter_context(tc.tile_pool(name="rows", bufs=3))
        packed = ctx.enter_context(tc.tile_pool(name="packed", bufs=6))
        results = ctx.enter_context(tc.tile_pool(name="results", bufs=4))
        spread = ctx.enter_context(tc.psum_pool(name="spread", bufs=2))
        sums = ctx.enter_context(tc.psum_pool(name="sums", bufs=4))

        th = const.tile([P, TILES, 2], BF16)
        nc.sync.dma_start(out=th[:], in_=theta.rearrange("(p i) two -> p i two", i=TILES))
        bs = const.tile([P, PASSES, PACK], BF16)
        nc.sync.dma_start(out=bs[:], in_=basis_sigma.rearrange("(c p t) -> p c t", p=P, t=PACK))
        bm = const.tile([P, PASSES, PACK], BF16)
        nc.sync.dma_start(out=bm[:], in_=basis_mu.rearrange("(c p t) -> p c t", p=P, t=PACK))
        raws = []
        for c in range(PASSES):
            raw = logs.tile([P, PACK, D], BF16, tag="ll", align_bytes=64)
            nc.sync.dma_start(
                out=raw[:],
                in_=Bv[c * P * PACK : (c + 1) * P * PACK, :].rearrange("(p t) w -> p t w", t=PACK),
            )
            raws.append(raw)

        ident = const.tile([P, P], F32)
        make_identity(nc, ident[:])
        identb = const.tile([P, P], BF16)
        make_identity(nc, identb[:])

        warm = const.tile([P, 1], F32)
        nc.vector.memset(warm[:], 1.0)
        warm2 = const.tile([P, 1], F32)
        nc.scalar.activation(out=warm2[:], in_=warm[:], func=AF.Ln)
        cofq = const.tile([P, 2 * PLANES, P], BF16)
        nc.vector.memset(cofq[:].bitcast(I32), 0)
        rowq = const.tile([P, TILES, P], BF16)
        for h0, h1 in FED_RUNS:
            nc.vector.memset(rowq[:, h0 * CHUNK_TILES : h1 * CHUNK_TILES, :].bitcast(I32), 0)

        rec = const.tile([P, TILES], F32)
        nc.vector.reciprocal(out=rec[:], in_=th[:, :, 1])
        mu = const.tile([P, TILES], F32)
        nc.vector.scalar_tensor_tensor(
            out=mu[:], in0=rec[:], scalar=-0.5 * kappa, in1=th[:, :, 0], op0=ALU.mult, op1=ALU.mult
        )
        bsf = bs[:].rearrange("p c t -> p (c t)")
        b2 = const.tile([P, PASSES * PACK], F32)
        nc.vector.scalar_tensor_tensor(
            out=b2[:], in0=bsf, scalar=2.0 * math.pi, in1=bsf, op0=ALU.mult, op1=ALU.mult
        )
        bmf = const.tile([P, PASSES * PACK], F32)
        nc.vector.tensor_scalar_mul(out=bmf[:], in0=bm[:].rearrange("p c t -> p (c t)"), scalar1=kappa)

        bvc = const.tile([P, PASSES, D], U32, align_bytes=64)
        bvs = const.tile([P, PASSES, D], U8, align_bytes=64)

        recb, mub, ll, ww, rb, cod, scl, acc, ost, grp = {}, {}, {}, {}, {}, {}, {}, {}, {}, {}
        d2, ss = {}, {}
        pi2 = math.pi * math.pi
        bmv = bm[:].rearrange("p c t -> p (c t)")
        rowsT = const.tile([P, len(FED) * CHUNK_TILES, P], BF16)
        cofT = const.tile([P, 2 * PLANES, P], BF16)
        kc = const.tile([P, 2 * PLANES], F32)

        def split3(src, shape, name):
            pieces = []
            rest = src
            for e in range(3):
                pc = const.tile(shape, BF16, name="%s_p%d" % (name, e))
                nc.vector.tensor_copy(out=pc[:], in_=rest[:])
                pieces.append(pc)
                if e < 2:
                    nxt = const.tile(shape, F32, name="%s_r%d" % (name, e))
                    nc.vector.tensor_tensor(out=nxt[:], in0=rest[:], in1=pc[:], op=ALU.subtract)
                    rest = nxt
            return pieces

        def prepare_rows():
            xf = const.tile([P, TERMS, TILES], F32)
            sg = const.tile([P, TILES], F32)
            nc.vector.tensor_scalar_mul(out=sg[:], in0=rec[:], scalar1=-0.5)
            nc.vector.tensor_scalar_mul(out=xf[:, 4, :], in0=rec[:], scalar1=-2.0 * pi2)
            nc.vector.scalar_tensor_tensor(
                out=xf[:, 3, :], in0=rec[:], scalar=4.0 * pi2, in1=th[:, :, 0], op0=ALU.mult, op1=ALU.mult
            )
            nc.vector.scalar_tensor_tensor(
                out=xf[:, 1, :], in0=xf[:, 3, :], scalar=1.0 / (16.0 * pi2), in1=xf[:, 3, :], op0=ALU.mult, op1=ALU.mult
            )
            nc.vector.tensor_tensor(out=xf[:, 0, :], in0=xf[:, 1, :], in1=sg[:], op=ALU.mult)
            nc.vector.tensor_tensor(out=xf[:, 2, :], in0=xf[:, 3, :], in1=sg[:], op=ALU.mult)
            nc.vector.tensor_scalar_mul(out=xf[:, 5, :], in0=xf[:, 1, :], scalar1=0.5 / math.pi)
            nc.vector.tensor_scalar_mul(out=xf[:, 6, :], in0=xf[:, 3, :], scalar1=0.5 / math.pi)
            pcs = split3(xf, [P, TERMS, TILES], "xf")
            for blk, (e, f) in enumerate(COMBOS):
                nc.vector.tensor_copy(
                    out=rowq[:, :, blk * SLOT : blk * SLOT + TERMS], in_=pcs[e][:].rearrange("p f i -> p i f")
                )

        def prepare_coefficients():
            cf = const.tile([P, TERMS, 2 * PLANES], F32)
            nc.vector.memset(cf[:], 0.0)
            lo = slice(0, PLANES)
            hi = slice(PLANES, 2 * PLANES)
            gg = const.tile([P, PLANES], F32)
            nc.vector.tensor_tensor(out=gg[:], in0=bsf, in1=bsf, op=ALU.mult)
            nc.vector.memset(cf[:, 0, lo], 1.0)
            nc.vector.memset(cf[:, 5, hi], 1.0)
            nc.vector.tensor_copy(out=cf[:, 6, hi], in_=bmv)
            nc.vector.tensor_tensor(out=kc[:, hi], in0=bmf[:], in1=bmf[:], op=ALU.mult)
            cfp = cf[:, 1, lo].rearrange("p (q two) -> p q two", two=2)
            ggp = gg[:].rearrange("p (q two) -> p q two", two=2)
            nc.vector.tensor_copy(out=cfp[:, :, 0], in_=ggp[:, :, 1])
            nc.vector.tensor_copy(out=cfp[:, :, 1], in_=ggp[:, :, 0])
            nc.vector.tensor_copy(out=cf[:, 2, lo], in_=bmv)
            nc.vector.tensor_tensor(out=cf[:, 3, lo], in0=cf[:, 2, lo], in1=cf[:, 1, lo], op=ALU.mult)
            nc.vector.tensor_tensor(out=cf[:, 4, lo], in0=cf[:, 2, lo], in1=cf[:, 2, lo], op=ALU.mult)
            nc.vector.scalar_tensor_tensor(
                out=kc[:, lo], in0=cf[:, 4, lo], scalar=4.0 * pi2, in1=cf[:, 1, lo], op0=ALU.mult, op1=ALU.mult
            )
            pcs = split3(cf, [P, TERMS, 2 * PLANES], "cf")
            for blk, (e, f) in enumerate(COMBOS):
                nc.vector.tensor_copy(
                    out=cofq[:, :, blk * SLOT : blk * SLOT + TERMS], in_=pcs[f][:].rearrange("p f k -> p k f")
                )

        def turn(dst, d0, src, s0):
            tp = sums.tile([P, 4, P], BF16, tag="acc")
            for j in range(4):
                nc.tensor.transpose(tp[:, j, :], src[:, s0 + j, :], identb[:])
            nc.vector.tensor_copy(out=dst[:, d0 : d0 + 4, :], in_=tp[:])

        def prepare_squares(part):
            if part == 0:
                prepare_coefficients()
                prepare_rows()
            for j0 in range(0, 2 * PLANES, 4):
                if (j0 >= PLANES) == (part == 0):
                    turn(cofT, j0, cofq, j0)
            for hh in range(len(FED)):
                if (FED[hh] < GROUP // 2) == (part == 0):
                    turn(rowsT, hh * CHUNK_TILES, rowq, FED[hh] * CHUNK_TILES)

        for st in plan():
            kind = st[0]
            if kind == "BR" or kind == "BM":
                h = st[1]
                src = rec if kind == "BR" else mu
                bk = spread.tile([P, BANK], F32, tag=kind)
                for a in range(CHUNK_TILES):
                    i = h * CHUNK_TILES + a
                    nc.tensor.transpose(bk[:, a * P : (a + 1) * P], src[:, i : i + 1].to_broadcast([P, P]), ident[:])
                if kind == "BR" and LN_FROM_SBUF:
                    rc = flat.tile([P, BANK], F32)
                    nc.vector.tensor_copy(out=rc[:], in_=bk[:])
                    recb[h] = rc
                elif kind == "BR":
                    recb[h] = bk
                else:
                    mub[h] = bk
            elif kind == "LN":
                u = st[1]
                lt = logs.tile([P, PACK, CHUNK], F32, tag="ll", align_bytes=64)
                for t in range(PACK):
                    k = (u % 2) * PACK + t
                    nc.scalar.activation(
                        out=lt[:, t, :],
                        in_=recb[u // 2][:],
                        func=AF.Ln,
                        bias=b2[:, k : k + 1],
                        scale=-math.pi,
                    )
                ll[u] = lt
            elif kind == "S":
                u = st[1]
                sst = pair.tile([P, PACK // 2, CHUNK], F32)
                lv = ll[u][:].rearrange("p (q two) n -> p q two n", two=2)
                if u in S_ON_DVE:
                    nc.vector.tensor_tensor(out=sst[:], in0=lv[:, :, 0, :], in1=lv[:, :, 1, :], op=ALU.add)
                else:
                    nc.gpsimd.tensor_tensor(out=sst[:], in0=lv[:, :, 0, :], in1=lv[:, :, 1, :], op=ALU.add)
                ss[u] = sst
            elif kind == "W":
                u = st[1]
                wt = work.tile([P, PACK, CHUNK], F32, tag="ww", align_bytes=64)
                ww[u] = wt
                if u // 2 in PAIRED:
                    sf = ss[u][:].rearrange("p q n -> p (q n)")
                    nc.scalar.activation(out=sf, in_=sf, func=AF.Exp, scale=-1.0)
                else:
                    nc.scalar.activation(
                        out=wt[:].rearrange("p t n -> p (t n)"),
                        in_=ll[u][:].rearrange("p t n -> p (t n)"),
                        func=AF.Exp,
                        scale=-1.0,
                    )
            elif kind == "A1" or kind == "B2":
                u = st[1]
                for t in range(PACK):
                    k = (u % 2) * PACK + t
                    nc.vector.scalar_tensor_tensor(
                        out=ww[u][:, t, :],
                        in0=mub[u // 2][:],
                        scalar=bmf[:, k : k + 1],
                        in1=ww[u][:, t, :],
                        op0=ALU.subtract,
                        op1=ALU.mult,
                    )
            elif kind == "PREP":
                prepare_squares(st[1])
            elif kind == "D2":
                u, t = st[1], st[2]
                k = (u % 2) * PACK + t
                d2t = spread.tile([P, BANK], F32, tag="BM")
                n0 = FED.index(u // 2) * CHUNK_TILES
                nc.tensor.matmul(
                    out=d2t[:],
                    lhsT=cofT[:, k if u // 2 in PAIRED else PLANES + k, :],
                    rhs=rowsT[:, n0 : n0 + CHUNK_TILES, :].rearrange("r a p -> r (a p)"),
                    start=True,
                    stop=True,
                )
                d2[(u, t)] = d2t
            elif kind == "BDV":
                u, t = st[1], st[2]
                k = (u % 2) * PACK + t
                kk = k if u // 2 in PAIRED else PLANES + k
                nc.vector.scalar_tensor_tensor(
                    out=ww[u][:, t, :],
                    in0=d2[(u, t)][:],
                    scalar=kc[:, kk : kk + 1],
                    in1=ss[u][:, t // 2, :] if u // 2 in PAIRED else ww[u][:, t, :],
                    op0=ALU.add,
                    op1=ALU.mult,
                )
            elif kind == "H":
                jk = const.tile([P, 1], U32, name="junk")
                nc.gpsimd.tensor_copy(out=jk[:], in_=cod[st[1]][:, 0:1])
            elif kind == "Z":
                u = st[1]
                wf = ww[u][:].rearrange("p t n -> p (t n)")
                lf = ll[u][:].rearrange("p t n -> p (t n)")
                if st[2] == "pool":
                    nc.gpsimd.tensor_tensor(out=wf, in0=wf, in1=lf, op=ALU.add)
                else:
                    nc.vector.tensor_tensor(out=wf, in0=wf, in1=lf, op=ALU.add)
            elif kind == "F":
                u = st[1]
                cols = slice(st[2] * P, st[3] * P)
                if u not in rb:
                    rbt = rows.tile([P, CHUNK, PACK], BF16, align_bytes=64)
                    rb[u] = rbt
                nc.scalar.activation(
                    out=rb[u][:, cols, :].rearrange("p (m i) t -> p m t i", i=4),
                    in_=ww[u][:, :, cols].rearrange("p t (m i) -> p m t i", i=4),
                    func=AF.Exp,
                    scale=-0.5,
                )
            elif kind == "Q":
                u = st[1]
                cols = slice(st[2] * P, st[3] * P)
                if u not in cod:
                    cdt = packed.tile([P, CHUNK], U32, align_bytes=64)
                    sct = packed.tile([P, CHUNK], U8, align_bytes=64)
                    cod[u], scl[u] = cdt, sct
                nc.vector.quantize_mx(
                    out=cod[u][:, cols].bitcast(FP8X4),
                    scales=scl[u][:, cols],
                    in_=rb[u][:, cols, :].rearrange("p n t -> p (n t)"),
                )
            elif kind == "BVG":
                c = st[1]
                gt = work.tile([P, D, PACK], BF16, tag="ww", align_bytes=64)
                nc.vector.tensor_copy(
                    out=gt[:].rearrange("p (m i) t -> p m t i", i=4),
                    in_=raws[c][:].rearrange("p t (m i) -> p m t i", i=4),
                )
                grp[c] = gt
            elif kind == "BVQ":
                c = st[1]
                nc.vector.quantize_mx(
                    out=bvc[:, c, :].bitcast(FP8X4),
                    scales=bvs[:, c, :],
                    in_=grp[c][:].rearrange("p w t -> p (w t)"),
                )
            elif kind == "MX":
                h, a = st[1], st[2]
                cols = slice(a * P, (a + 1) * P)
                for dh in range(D // BANK):
                    if st[3] == "acc":
                        at = sums.tile([P, BANK], F32, tag="acc")
                    else:
                        at = spread.tile([P, BANK], F32, tag=st[3])
                    dcols = slice(dh * BANK, (dh + 1) * BANK)
                    for c in range(PASSES):
                        nc.tensor.matmul_mx(
                            out=at[:],
                            lhsT=cod[2 * h + c][:, cols].bitcast(FP8X4),
                            lhsT_scale=scl[2 * h + c][:, cols],
                            rhs=bvc[:, c, dcols].bitcast(FP8X4),
                            rhs_scale=bvs[:, c, dcols],
                            start=(c == 0),
                            stop=(c == PASSES - 1),
                        )
                    acc[(h, a, dh)] = at
            elif kind == "EV":
                h, a, dh, eng = st[1], st[2], st[3], st[4]
                if (h, a // 2) not in ost:
                    ot = results.tile([P, 2, D], F32)
                    ost[(h, a // 2)] = ot
                dst = ost[(h, a // 2)][:, a % 2, dh * BANK : (dh + 1) * BANK]
                if eng == "act":
                    nc.scalar.copy(out=dst, in_=acc[(h, a, dh)][:])
                else:
                    nc.vector.tensor_copy(out=dst, in_=acc[(h, a, dh)][:])
            elif kind == "ST":
                h, a0, a1 = st[1], st[2], st[3]
                i0 = h * CHUNK_TILES
                nc.sync.dma_start(
                    out=out_v[:, i0 + a0 : i0 + a1, :], in_=ost[(h, a0 // 2)][:, a0 % 2 : a0 % 2 + a1 - a0, :]
                )
